import numpy as np
import ml_dtypes


def mxq(x, axis, fmt="e4m3"):
    dtype, down = {"e4m3": (ml_dtypes.float8_e4m3fn, 7), "e5m2": (ml_dtypes.float8_e5m2, 14)}[fmt]
    v = np.moveaxis(np.asarray(x, np.float32).astype(ml_dtypes.bfloat16).astype(np.float64), axis, -1)
    blocks = v.reshape(v.shape[:-1] + (-1, 32))
    amax = np.abs(blocks).max(-1, keepdims=True)
    byte = np.maximum(np.where(amax > 0, np.frexp(amax)[1] - 1 + 127, 0) - down, 1)
    scale = np.exp2(byte - 127.0)
    codes = (blocks / scale).astype(np.float32).astype(dtype).astype(np.float64)
    return np.moveaxis((codes * scale).reshape(v.shape), -1, axis)


WIDE = False


def mx_kscale(k):
    if not WIDE:
        return np.ones(k)
    levels = np.array([10, -10, 5, -5, 0])
    a = np.random.permutation(np.resize(levels, k // 512 * 4)).reshape(k // 512, 4)
    idx = np.arange(k)
    return np.exp2(a[idx // 512, idx % 128 // 32])


BF16 = ml_dtypes.bfloat16


def bf(x):
    return np.asarray(x, np.float32).astype(BF16)


def f64(x):
    return np.asarray(x).astype(np.float64)


S, NF, HID, T = 64, 128, 1024, 128
FIN = 8 * NF


def silu(v):
    e = np.exp(-np.abs(v))
    return v * np.where(v >= 0.0, 1.0, e) / (1.0 + e)


def fourier_features(dr, dc, freqs):
    f = freqs[None, None, :]
    a = dr[..., None] * f
    b = dc[..., None] * f
    p = (dr + dc)[..., None] * f
    m = (dr - dc)[..., None] * f
    return np.concatenate([np.sin(a), np.cos(a), np.sin(b), np.cos(b),
                           np.sin(p), np.cos(p), np.sin(m), np.cos(m)], axis=-1)


def setup_inputs():
    r = np.sqrt(S) - 1.0
    t = mx_kscale(HID)
    u = t / np.min(t)
    freqs = np.exp(np.linspace(np.log(1.0), np.log(1.0 / 50.0), NF)) * (1.0 + 0.1 * np.random.standard_normal(NF))
    return {"seq_len": S,
            "freqs": bf(freqs),
            "W1": bf(np.random.standard_normal((HID, FIN)) * 1.5 / np.sqrt(FIN) * u[:, None]),
            "b1": bf(np.random.standard_normal(HID) * 0.3 * u),
            "W2": bf(np.random.standard_normal((T, HID)) * 1.6 * T ** 0.25 / np.sqrt(HID) / u[None, :]),
            "b2": bf(np.random.standard_normal(T) * 0.3 * T ** 0.25),
            "dr": bf(np.random.uniform(-r, r, (S, S))),
            "dc": bf(np.random.uniform(-r, r, (S, S)))}


def reference(seq_len, freqs, W1, b1, W2, b2, dr, dc):
    dr_s = f64(dr)[:seq_len, :seq_len]
    dc_s = f64(dc)[:seq_len, :seq_len]
    feats = fourier_features(dr_s, dc_s, f64(freqs))
    h = silu((mxq(feats, 2, "e4m3") @ mxq(f64(W1), 1, "e4m3").T) + f64(b1))
    out = (mxq(h, 2, "e4m3") @ mxq(f64(W2), 1, "e4m3").T) + f64(b2)
    return out * (1.0 / np.sqrt(T))

@@ -1,0 +1,208 @@
+from contextlib import ExitStack
+import math
+
+import concourse.bass as bass
+import concourse.mybir as mybir
+import concourse.tile as tile
+from concourse.masks import make_identity
+
+F32 = mybir.dt.float32
+BF16 = mybir.dt.bfloat16
+I32 = mybir.dt.int32
+U32 = mybir.dt.uint32
+U8 = mybir.dt.uint8
+FP8X4 = mybir.dt.float8_e4m3fn_x4
+ALU = mybir.AluOpType
+ACT = mybir.ActivationFunctionType
+
+P = 128
+PAIRS = 4096
+NT = 8
+SUB = 4
+HID = 1024
+MT = 8
+T = 128
+FLOPS = 2 * PAIRS * 1024 * HID + 2 * PAIRS * HID * T
+
+INV_2PI = 1.0 / (2.0 * math.pi)
+TWO_PI = 2.0 * math.pi
+OUT_SCALE = 1.0 / math.sqrt(128.0)
+ABS_DVE_COLS = 1024
+
+
+def tile_gabtemplatemlp_t_kernel(tc, seq_len, freqs, W1, b1, W2, b2, dr, dc, out):
+    nc = tc.nc
+    with ExitStack() as ctx:
+        const = ctx.enter_context(tc.tile_pool(name="const", bufs=1))
+        work = ctx.enter_context(tc.tile_pool(name="work", bufs=2))
+        ps_th = ctx.enter_context(tc.psum_pool(name="ps_th", bufs=2))
+        ps_z = ctx.enter_context(tc.psum_pool(name="ps_z", bufs=4))
+        ps_o = ctx.enter_context(tc.psum_pool(name="ps_o", bufs=2))
+
+        dd = const.tile([P, 512], BF16)
+        nc.vector.memset(dd[:], 0.0)
+        nc.sync.dma_start(out=dd[0:8, :], in_=dr.rearrange("i j -> (i j)").rearrange("(a n) -> a n", n=512))
+        nc.sync.dma_start(out=dd[32:40, :], in_=dc.rearrange("i j -> (i j)").rearrange("(a n) -> a n", n=512))
+        fb = const.tile([P, P], BF16)
+        nc.sync.dma_start(out=fb[:], in_=freqs.partition_broadcast(P))
+        w1raw = const.tile([P, 32, 256], BF16)
+        w1v = W1.rearrange("h f -> (h f)").rearrange("(b q x) -> q b x", q=P, x=256)
+        for part in range(4):
+            nc.sync.dma_start(out=w1raw[:, 8 * part:8 * part + 8, :], in_=w1v[:, 8 * part:8 * part + 8, :])
+        brow = const.tile([P, P], BF16)
+        nc.vector.memset(brow[:], 0.0)
+        nc.sync.dma_start(out=brow[0:8, :], in_=b1.rearrange("(j p) -> j p", p=P))
+        w2raw = const.tile([P, HID], BF16)
+        nc.sync.dma_start(out=w2raw[:], in_=W2)
+        b2b = const.tile([P, T], BF16)
+        nc.sync.dma_start(out=b2b[:], in_=b2.partition_broadcast(P))
+
+        warm = const.tile([P, 1], F32)
+        nc.vector.memset(warm[:], 0.0)
+        nc.scalar.activation(out=warm[:], in_=warm[:], func=ACT.Silu)
+        one = const.tile([P, 1], F32)
+        nc.vector.memset(one[:], 1.0)
+        halfpi = const.tile([P, 1], F32)
+        nc.vector.tensor_scalar(out=halfpi[:], in0=one[:], scalar1=math.pi / 2.0, scalar2=None, op0=ALU.mult)
+        ident = const.tile([P, P], BF16)
+        make_identity(nc, ident[:])
+        coef = const.tile([P, 4], BF16)
+        nc.vector.memset(coef[:], 0.0)
+        nc.vector.memset(coef[0:32, 0:1], 1.0)
+        nc.vector.memset(coef[0:32, 2:4], 1.0)
+        nc.vector.memset(coef[32:64, 1:3], 1.0)
+        nc.vector.memset(coef[32:64, 3:4], -1.0)
+        mask = const.tile([P, NT], BF16)
+        nc.vector.tensor_tensor(out=mask[:], in0=ident[:, 0:NT], in1=ident[:, 32:32 + NT], op=ALU.add)
+        lsel = const.tile([P, NT, P], BF16)
+        nc.vector.tensor_tensor(
+            out=lsel[:],
+            in0=fb[:].unsqueeze(1).to_broadcast([P, NT, P]),
+            in1=mask[:].unsqueeze(2).to_broadcast([P, NT, P]),
+            op=ALU.mult,
+        )
+        xmov = const.tile([P, SUB, P, 4], BF16)
+        ddv = dd[:].rearrange("k (n s) -> k s n", s=SUB)
+        for s in range(SUB):
+            nc.vector.tensor_tensor(
+                out=xmov[:, s, :, :],
+                in0=ddv[:, s, :].unsqueeze(2).to_broadcast([P, P, 4]),
+                in1=coef[:].unsqueeze(1).to_broadcast([P, P, 4]),
+                op=ALU.mult,
+            )
+
+        fcodes = const.tile([P, 2, NT, 512], U32, align_bytes=64)
+        fscales = const.tile([P, 2, NT, 512], U8, align_bytes=64)
+        w1c = const.tile([P, 2, HID], U32, align_bytes=64)
+        w1s = const.tile([P, 2, HID], U8, align_bytes=64)
+        w2c = const.tile([P, 2, T], U32, align_bytes=64)
+        w2s = const.tile([P, 2, T], U8, align_bytes=64)
+        b1c = const.tile([P, MT], F32)
+        b2s = const.tile([P, T], F32)
+
+        def features(nt):
+            r = work.tile([P, SUB, 512], F32, tag="r", bufs=3)
+            for s in range(SUB):
+                th = ps_th.tile([P, 512], F32, tag="th")
+                nc.tensor.matmul(out=th[:], lhsT=lsel[:, nt, :], rhs=xmov[:, s, :, :].rearrange("k n t -> k (n t)"),
+                                 start=True, stop=True)
+                kk = work.tile([P, 512], I32, tag="kk", bufs=4)
+                nc.vector.tensor_scalar(out=kk[:], in0=th[:], scalar1=INV_2PI, scalar2=None, op0=ALU.mult)
+                nc.vector.scalar_tensor_tensor(out=r[:, s, :], in0=th[:], scalar=INV_2PI, in1=kk[:],
+                                               op0=ALU.mult, op1=ALU.subtract)
+            rf = r[:].rearrange("p s c -> p (s c)")
+            fs = work.tile([P, 2048], BF16, tag="fs", align_bytes=64)
+            nc.scalar.activation(out=fs[:], in_=rf, func=ACT.Sin, scale=TWO_PI)
+            ab = work.tile([P, 2048], F32, tag="ab")
+            nc.vector.scalar_tensor_tensor(out=ab[:, 0:ABS_DVE_COLS], in0=rf[:, 0:ABS_DVE_COLS], scalar=-1.0,
+                                           in1=rf[:, 0:ABS_DVE_COLS], op0=ALU.mult, op1=ALU.max)
+            nc.scalar.activation(out=ab[:, ABS_DVE_COLS:2048], in_=rf[:, ABS_DVE_COLS:2048], func=ACT.Abs)
+            fc = work.tile([P, 2048], BF16, tag="fc", align_bytes=64)
+            nc.scalar.activation(out=fc[:], in_=ab[:], func=ACT.Sin, scale=-TWO_PI, bias=halfpi[:])
+            nc.vector.quantize_mx(out=fcodes[:, 0, nt, :].bitcast(FP8X4), scales=fscales[:, 0, nt, :], in_=fs[:])
+            nc.vector.quantize_mx(out=fcodes[:, 1, nt, :].bitcast(FP8X4), scales=fscales[:, 1, nt, :], in_=fc[:])
+
+        def weights():
+            bt = ps_z.tile([P, P], BF16, tag="z")
+            nc.tensor.transpose(out=bt[:], in_=brow[:], identity=ident[:])
+            nc.vector.tensor_copy(out=b1c[:], in_=bt[:, 0:MT])
+            nc.vector.tensor_scalar(out=b2s[:], in0=b2b[:], scalar1=OUT_SCALE, scalar2=None, op0=ALU.mult)
+            for j in range(MT):
+                for sp in range(2):
+                    wt = ps_z.tile([P, 512], BF16, tag="z")
+                    for b in range(4):
+                        nc.tensor.transpose(out=wt[:, P * b:P * b + P],
+                                            in_=w1raw[:, 4 * j + b, P * sp:P * sp + P], identity=ident[:])
+                    wg = work.tile([P, 512], BF16, tag="wg", bufs=4, align_bytes=64)
+                    nc.scalar.copy(out=wg[:], in_=wt[:])
+                    nc.vector.quantize_mx(out=w1c[:, sp, P * j:P * j + P].bitcast(FP8X4),
+                                          scales=w1s[:, sp, P * j:P * j + P], in_=wg[:])
+            for g in range(2):
+                w2t = ps_z.tile([P, 4, P], BF16, tag="z")
+                for t in range(4):
+                    nc.tensor.transpose(out=w2t[:, t, :], in_=w2raw[:, P * (4 * g + t):P * (4 * g + t) + P],
+                                        identity=ident[:])
+                w2g = work.tile([P, P, 4], BF16, tag="wg", bufs=4, align_bytes=64)
+                nc.vector.tensor_copy(out=w2g[:], in_=w2t[:].rearrange("p t c -> p c t"))
+                nc.vector.quantize_mx(out=w2c[:, g, :].bitcast(FP8X4), scales=w2s[:, g, :],
+                                      in_=w2g[:].rearrange("p c t -> p (c t)"))
+
+        def stage1(nt):
+            hpl = work.tile([P, MT, 512], BF16, tag="hpl")
+            hc = work.tile([P, 2, 512], U32, tag="hc", align_bytes=64)
+            hs = work.tile([P, 2, 512], U8, tag="hs", align_bytes=64)
+            for g in range(2):
+                for t in range(4):
+                    j = 4 * g + t
+                    z = ps_z.tile([P, 512], F32, tag="z")
+                    for sp in range(2):
+                        nc.tensor.matmul_mx(
+                            out=z[:],
+                            lhsT=w1c[:, sp, P * j:P * j + P].bitcast(FP8X4),
+                            lhsT_scale=w1s[:, sp, P * j:P * j + P],
+                            rhs=fcodes[:, sp, nt, :].bitcast(FP8X4),
+                            rhs_scale=fscales[:, sp, nt, :],
+                            start=(sp == 0), stop=(sp == 1),
+                        )
+                    nc.scalar.activation(out=hpl[:, j, :], in_=z[:], func=ACT.Silu, bias=b1c[:, j:j + 1])
+                hg = work.tile([P, 512, 4], BF16, tag="hg", bufs=3, align_bytes=64)
+                nc.vector.tensor_copy(
+                    out=hg[:].rearrange("p (c i) t -> p c t i", i=4),
+                    in_=hpl[:, 4 * g:4 * g + 4, :].rearrange("p t (c i) -> p c t i", i=4),
+                )
+                nc.vector.quantize_mx(out=hc[:, g, :].bitcast(FP8X4), scales=hs[:, g, :],
+                                      in_=hg[:].rearrange("p w t -> p (w t)"))
+            return hc, hs
+
+        outv = out.rearrange("i j t -> (i j) t").rearrange("(a n s) t -> a n (s t)", n=P, s=SUB)
+
+        def stage2(nt, hc, hs):
+            o = ps_o.tile([P, SUB, T], F32, tag="o")
+            for s in range(SUB):
+                for g in range(2):
+                    nc.tensor.matmul_mx(
+                        out=o[:, s, :],
+                        lhsT=hc[:, g, P * s:P * s + P].bitcast(FP8X4),
+                        lhsT_scale=hs[:, g, P * s:P * s + P],
+                        rhs=w2c[:, g, :].bitcast(FP8X4),
+                        rhs_scale=w2s[:, g, :],
+                        start=(g == 0), stop=(g == 1),
+                    )
+            osb = work.tile([P, SUB, T], F32, tag="osb", bufs=3)
+            nc.vector.scalar_tensor_tensor(out=osb[:], in0=o[:], scalar=OUT_SCALE,
+                                           in1=b2s[:].unsqueeze(1).to_broadcast([P, SUB, T]),
+                                           op0=ALU.mult, op1=ALU.add)
+            nc.sync.dma_start(out=outv[nt], in_=osb[:].rearrange("p s t -> p (s t)"))
+
+        features(0)
+        weights()
+        features(1)
+        prev = None
+        for nt in range(NT):
+            if nt + 2 < NT:
+                features(nt + 2)
+            cur = stage1(nt)
+            if prev is not None:
+                stage2(nt - 1, prev[0], prev[1])
+            prev = cur
+        stage2(NT - 1, prev[0], prev[1])

@@ -1,9 +1,7 @@
 from contextlib import ExitStack
 import math
 
-import concourse.bass as bass
 import concourse.mybir as mybir
-import concourse.tile as tile
 from concourse.masks import make_identity
 
 F32 = mybir.dt.float32
@@ -19,6 +17,7 @@ P = 128
 PAIRS = 4096
 NT = 8
 SUB = 4
+NCH = NT * SUB
 HID = 1024
 MT = 8
 T = 128
@@ -27,17 +26,28 @@ FLOPS = 2 * PAIRS * 1024 * HID + 2 * PAIRS * HID * T
 INV_2PI = 1.0 / (2.0 * math.pi)
 TWO_PI = 2.0 * math.pi
 OUT_SCALE = 1.0 / math.sqrt(128.0)
-ABS_DVE_COLS = 1024
+
+PIN = False
+ABS_DVE_EVERY = 3
+TH_BUFS = 3
+Z_BUFS = 4
+O_BUFS = 1
+TH_LEAD = 2
+W_SLOT0 = 2
+W_PER_SLOT = 4
+MLP_LAG = 7
 
 
 def tile_gabtemplatemlp_t_kernel(tc, seq_len, freqs, W1, b1, W2, b2, dr, dc, out):
     nc = tc.nc
     with ExitStack() as ctx:
+        if PIN:
+            ctx.enter_context(tc.manual_schedule())
         const = ctx.enter_context(tc.tile_pool(name="const", bufs=1))
         work = ctx.enter_context(tc.tile_pool(name="work", bufs=2))
-        ps_th = ctx.enter_context(tc.psum_pool(name="ps_th", bufs=2))
-        ps_z = ctx.enter_context(tc.psum_pool(name="ps_z", bufs=4))
-        ps_o = ctx.enter_context(tc.psum_pool(name="ps_o", bufs=2))
+        ps_th = ctx.enter_context(tc.psum_pool(name="ps_th", bufs=TH_BUFS))
+        ps_z = ctx.enter_context(tc.psum_pool(name="ps_z", bufs=Z_BUFS))
+        ps_o = ctx.enter_context(tc.psum_pool(name="ps_o", bufs=O_BUFS))
 
         dd = const.tile([P, 512], BF16)
         nc.vector.memset(dd[:], 0.0)
@@ -60,12 +70,12 @@ def tile_gabtemplatemlp_t_kernel(tc, seq_len, freqs, W1, b1, W2, b2, dr, dc, out
         warm = const.tile([P, 1], F32)
         nc.vector.memset(warm[:], 0.0)
         nc.scalar.activation(out=warm[:], in_=warm[:], func=ACT.Silu)
+        ident = const.tile([P, P], BF16)
+        make_identity(nc, ident[:])
         one = const.tile([P, 1], F32)
         nc.vector.memset(one[:], 1.0)
         halfpi = const.tile([P, 1], F32)
         nc.vector.tensor_scalar(out=halfpi[:], in0=one[:], scalar1=math.pi / 2.0, scalar2=None, op0=ALU.mult)
-        ident = const.tile([P, P], BF16)
-        make_identity(nc, ident[:])
         coef = const.tile([P, 4], BF16)
         nc.vector.memset(coef[:], 0.0)
         nc.vector.memset(coef[0:32, 0:1], 1.0)
@@ -75,21 +85,31 @@ def tile_gabtemplatemlp_t_kernel(tc, seq_len, freqs, W1, b1, W2, b2, dr, dc, out
         mask = const.tile([P, NT], BF16)
         nc.vector.tensor_tensor(out=mask[:], in0=ident[:, 0:NT], in1=ident[:, 32:32 + NT], op=ALU.add)
         lsel = const.tile([P, NT, P], BF16)
-        nc.vector.tensor_tensor(
-            out=lsel[:],
-            in0=fb[:].unsqueeze(1).to_broadcast([P, NT, P]),
-            in1=mask[:].unsqueeze(2).to_broadcast([P, NT, P]),
-            op=ALU.mult,
-        )
         xmov = const.tile([P, SUB, P, 4], BF16)
         ddv = dd[:].rearrange("k (n s) -> k s n", s=SUB)
-        for s in range(SUB):
+
+        def build_x(s):
             nc.vector.tensor_tensor(
                 out=xmov[:, s, :, :],
                 in0=ddv[:, s, :].unsqueeze(2).to_broadcast([P, P, 4]),
                 in1=coef[:].unsqueeze(1).to_broadcast([P, P, 4]),
                 op=ALU.mult,
             )
+
+        def build_l(lo, hi):
+            nc.vector.tensor_tensor(
+                out=lsel[:, lo:hi, :],
+                in0=fb[:].unsqueeze(1).to_broadcast([P, hi - lo, P]),
+                in1=mask[:, lo:hi].unsqueeze(2).to_broadcast([P, hi - lo, P]),
+                op=ALU.mult,
+            )
+
+        build_x(0)
+        build_l(0, 1)
+        build_x(1)
+        build_x(2)
+        build_x(3)
+        build_l(1, NT)
 
         fcodes = const.tile([P, 2, NT, 512], U32, align_bytes=64)
         fscales = const.tile([P, 2, NT, 512], U8, align_bytes=64)
@@ -99,110 +119,187 @@ def tile_gabtemplatemlp_t_kernel(tc, seq_len, freqs, W1, b1, W2, b2, dr, dc, out
         w2s = const.tile([P, 2, T], U8, align_bytes=64)
         b1c = const.tile([P, MT], F32)
         b2s = const.tile([P, T], F32)
+        outv = out.rearrange("i j t -> (i j) t").rearrange("(a n s) t -> a n (s t)", n=P, s=SUB)
 
-        def features(nt):
-            r = work.tile([P, SUB, 512], F32, tag="r", bufs=3)
-            for s in range(SUB):
-                th = ps_th.tile([P, 512], F32, tag="th")
-                nc.tensor.matmul(out=th[:], lhsT=lsel[:, nt, :], rhs=xmov[:, s, :, :].rearrange("k n t -> k (n t)"),
-                                 start=True, stop=True)
-                kk = work.tile([P, 512], I32, tag="kk", bufs=4)
-                nc.vector.tensor_scalar(out=kk[:], in0=th[:], scalar1=INV_2PI, scalar2=None, op0=ALU.mult)
-                nc.vector.scalar_tensor_tensor(out=r[:, s, :], in0=th[:], scalar=INV_2PI, in1=kk[:],
-                                               op0=ALU.mult, op1=ALU.subtract)
-            rf = r[:].rearrange("p s c -> p (s c)")
-            fs = work.tile([P, 2048], BF16, tag="fs", align_bytes=64)
-            nc.scalar.activation(out=fs[:], in_=rf, func=ACT.Sin, scale=TWO_PI)
-            ab = work.tile([P, 2048], F32, tag="ab")
-            nc.vector.scalar_tensor_tensor(out=ab[:, 0:ABS_DVE_COLS], in0=rf[:, 0:ABS_DVE_COLS], scalar=-1.0,
-                                           in1=rf[:, 0:ABS_DVE_COLS], op0=ALU.mult, op1=ALU.max)
-            nc.scalar.activation(out=ab[:, ABS_DVE_COLS:2048], in_=rf[:, ABS_DVE_COLS:2048], func=ACT.Abs)
-            fc = work.tile([P, 2048], BF16, tag="fc", align_bytes=64)
-            nc.scalar.activation(out=fc[:], in_=ab[:], func=ACT.Sin, scale=-TWO_PI, bias=halfpi[:])
-            nc.vector.quantize_mx(out=fcodes[:, 0, nt, :].bitcast(FP8X4), scales=fscales[:, 0, nt, :], in_=fs[:])
-            nc.vector.quantize_mx(out=fcodes[:, 1, nt, :].bitcast(FP8X4), scales=fscales[:, 1, nt, :], in_=fc[:])
+        th = {}
+        rr = {}
+        ab = {}
+        feat = {}
+        zz = {}
+        hpl = {}
+        hgr = {}
+        hq = {}
+        oo = {}
+        wts = {}
 
-        def weights():
+        def theta(c):
+            th[c] = ps_th.tile([P, 512], F32, tag="th", name="th")
+            nc.tensor.matmul(out=th[c][:], lhsT=lsel[:, c // SUB, :],
+                             rhs=xmov[:, c % SUB, :, :].rearrange("k n t -> k (n t)"), start=True, stop=True)
+
+        def reduce(c):
+            kk = work.tile([P, 512], I32, tag="kk", bufs=3)
+            nc.vector.tensor_scalar(out=kk[:], in0=th[c][:], scalar1=INV_2PI, scalar2=None, op0=ALU.mult)
+            rr[c] = work.tile([P, 512], F32, tag="r", bufs=4, name="r")
+            nc.vector.scalar_tensor_tensor(out=rr[c][:], in0=th[c][:], scalar=INV_2PI, in1=kk[:],
+                                           op0=ALU.mult, op1=ALU.subtract)
+
+        def sin_s(c):
+            nt, s = c // SUB, c % SUB
+            if s == 0:
+                feat[(nt, 0)] = work.tile([P, 2048], BF16, tag="fs", bufs=3, align_bytes=64, name="fs")
+            nc.scalar.activation(out=feat[(nt, 0)][:, 512 * s:512 * s + 512], in_=rr[c][:], func=ACT.Sin, scale=TWO_PI)
+
+        def abs_on_dve(c):
+            return c % ABS_DVE_EVERY == ABS_DVE_EVERY - 1
+
+        def fold(c):
+            ab[c] = work.tile([P, 512], F32, tag="ab", bufs=4, name="ab")
+            if abs_on_dve(c):
+                nc.vector.scalar_tensor_tensor(out=ab[c][:], in0=rr[c][:], scalar=-1.0, in1=rr[c][:],
+                                               op0=ALU.mult, op1=ALU.max)
+            else:
+                nc.scalar.activation(out=ab[c][:], in_=rr[c][:], func=ACT.Abs)
+
+        def sin_c(c):
+            nt, s = c // SUB, c % SUB
+            if s == 0:
+                feat[(nt, 1)] = work.tile([P, 2048], BF16, tag="fc", bufs=3, align_bytes=64, name="fc")
+            nc.scalar.activation(out=feat[(nt, 1)][:, 512 * s:512 * s + 512], in_=ab[c][:], func=ACT.Sin,
+                                 scale=-TWO_PI, bias=halfpi[:])
+
+        def quant_f(nt, sp):
+            nc.vector.quantize_mx(out=fcodes[:, sp, nt, :].bitcast(FP8X4), scales=fscales[:, sp, nt, :],
+                                  in_=feat[(nt, sp)][:])
+
+        def w1_pe(u):
+            j, sp = u // 2, u % 2
+            wts[u] = ps_z.tile([P, 512], BF16, tag="z", name="wt")
+            for b in range(4):
+                nc.tensor.transpose(out=wts[u][:, P * b:P * b + P],
+                                    in_=w1raw[:, 4 * j + b, P * sp:P * sp + P], identity=ident[:])
+
+        def w1_exit(u):
+            wg = work.tile([P, 512], BF16, tag="wg", bufs=4, align_bytes=64)
+            nc.scalar.copy(out=wg[:], in_=wts[u][:])
+            wts[u] = wg
+
+        def w1_quant(u):
+            j, sp = u // 2, u % 2
+            nc.vector.quantize_mx(out=w1c[:, sp, P * j:P * j + P].bitcast(FP8X4),
+                                  scales=w1s[:, sp, P * j:P * j + P], in_=wts[u][:])
+
+        def small_weights():
             bt = ps_z.tile([P, P], BF16, tag="z")
             nc.tensor.transpose(out=bt[:], in_=brow[:], identity=ident[:])
             nc.vector.tensor_copy(out=b1c[:], in_=bt[:, 0:MT])
             nc.vector.tensor_scalar(out=b2s[:], in0=b2b[:], scalar1=OUT_SCALE, scalar2=None, op0=ALU.mult)
-            for j in range(MT):
-                for sp in range(2):
-                    wt = ps_z.tile([P, 512], BF16, tag="z")
-                    for b in range(4):
-                        nc.tensor.transpose(out=wt[:, P * b:P * b + P],
-                                            in_=w1raw[:, 4 * j + b, P * sp:P * sp + P], identity=ident[:])
-                    wg = work.tile([P, 512], BF16, tag="wg", bufs=4, align_bytes=64)
-                    nc.scalar.copy(out=wg[:], in_=wt[:])
-                    nc.vector.quantize_mx(out=w1c[:, sp, P * j:P * j + P].bitcast(FP8X4),
-                                          scales=w1s[:, sp, P * j:P * j + P], in_=wg[:])
+            w2g = {}
             for g in range(2):
                 w2t = ps_z.tile([P, 4, P], BF16, tag="z")
                 for t in range(4):
                     nc.tensor.transpose(out=w2t[:, t, :], in_=w2raw[:, P * (4 * g + t):P * (4 * g + t) + P],
                                         identity=ident[:])
-                w2g = work.tile([P, P, 4], BF16, tag="wg", bufs=4, align_bytes=64)
-                nc.vector.tensor_copy(out=w2g[:], in_=w2t[:].rearrange("p t c -> p c t"))
-                nc.vector.quantize_mx(out=w2c[:, g, :].bitcast(FP8X4), scales=w2s[:, g, :],
-                                      in_=w2g[:].rearrange("p c t -> p (c t)"))
-
-        def stage1(nt):
-            hpl = work.tile([P, MT, 512], BF16, tag="hpl")
-            hc = work.tile([P, 2, 512], U32, tag="hc", align_bytes=64)
-            hs = work.tile([P, 2, 512], U8, tag="hs", align_bytes=64)
+                w2g[g] = work.tile([P, P, 4], BF16, tag="w2g", bufs=2, align_bytes=64, name="w2g")
+                nc.vector.tensor_copy(out=w2g[g][:], in_=w2t[:].rearrange("p t c -> p c t"))
             for g in range(2):
-                for t in range(4):
-                    j = 4 * g + t
-                    z = ps_z.tile([P, 512], F32, tag="z")
-                    for sp in range(2):
-                        nc.tensor.matmul_mx(
-                            out=z[:],
-                            lhsT=w1c[:, sp, P * j:P * j + P].bitcast(FP8X4),
-                            lhsT_scale=w1s[:, sp, P * j:P * j + P],
-                            rhs=fcodes[:, sp, nt, :].bitcast(FP8X4),
-                            rhs_scale=fscales[:, sp, nt, :],
-                            start=(sp == 0), stop=(sp == 1),
-                        )
-                    nc.scalar.activation(out=hpl[:, j, :], in_=z[:], func=ACT.Silu, bias=b1c[:, j:j + 1])
-                hg = work.tile([P, 512, 4], BF16, tag="hg", bufs=3, align_bytes=64)
-                nc.vector.tensor_copy(
-                    out=hg[:].rearrange("p (c i) t -> p c t i", i=4),
-                    in_=hpl[:, 4 * g:4 * g + 4, :].rearrange("p t (c i) -> p c t i", i=4),
+                nc.vector.quantize_mx(out=w2c[:, g, :].bitcast(FP8X4), scales=w2s[:, g, :],
+                                      in_=w2g[g][:].rearrange("p c t -> p (c t)"))
+
+        def mm1(nt, j):
+            zz[(nt, j)] = ps_z.tile([P, 512], F32, tag="z", name="z")
+            for sp in range(2):
+                nc.tensor.matmul_mx(
+                    out=zz[(nt, j)][:],
+                    lhsT=w1c[:, sp, P * j:P * j + P].bitcast(FP8X4),
+                    lhsT_scale=w1s[:, sp, P * j:P * j + P],
+                    rhs=fcodes[:, sp, nt, :].bitcast(FP8X4),
+                    rhs_scale=fscales[:, sp, nt, :],
+                    start=(sp == 0), stop=(sp == 1),
                 )
-                nc.vector.quantize_mx(out=hc[:, g, :].bitcast(FP8X4), scales=hs[:, g, :],
-                                      in_=hg[:].rearrange("p w t -> p (w t)"))
-            return hc, hs
 
-        outv = out.rearrange("i j t -> (i j) t").rearrange("(a n s) t -> a n (s t)", n=P, s=SUB)
+        def silu(nt, j):
+            if j == 0:
+                hpl[nt] = work.tile([P, MT, 512], BF16, tag="hpl", bufs=2, name="hpl")
+            nc.scalar.activation(out=hpl[nt][:, j, :], in_=zz[(nt, j)][:], func=ACT.Silu, bias=b1c[:, j:j + 1])
 
-        def stage2(nt, hc, hs):
-            o = ps_o.tile([P, SUB, T], F32, tag="o")
+        def regroup(nt, g):
+            hgr[(nt, g)] = work.tile([P, 512, 4], BF16, tag="hg", bufs=3, align_bytes=64, name="hg")
+            nc.vector.tensor_copy(
+                out=hgr[(nt, g)][:].rearrange("p (c i) t -> p c t i", i=4),
+                in_=hpl[nt][:, 4 * g:4 * g + 4, :].rearrange("p t (c i) -> p c t i", i=4),
+            )
+
+        def quant_h(nt, g):
+            if g == 0:
+                hq[nt] = (work.tile([P, 2, 512], U32, tag="hc", bufs=2, align_bytes=64, name="hc"),
+                          work.tile([P, 2, 512], U8, tag="hs", bufs=2, align_bytes=64, name="hs"))
+            nc.vector.quantize_mx(out=hq[nt][0][:, g, :].bitcast(FP8X4), scales=hq[nt][1][:, g, :],
+                                  in_=hgr[(nt, g)][:].rearrange("p w t -> p (w t)"))
+
+        def mm2(nt):
+            oo[nt] = ps_o.tile([P, SUB, T], F32, tag="o", name="o")
             for s in range(SUB):
                 for g in range(2):
                     nc.tensor.matmul_mx(
-                        out=o[:, s, :],
-                        lhsT=hc[:, g, P * s:P * s + P].bitcast(FP8X4),
-                        lhsT_scale=hs[:, g, P * s:P * s + P],
+                        out=oo[nt][:, s, :],
+                        lhsT=hq[nt][0][:, g, P * s:P * s + P].bitcast(FP8X4),
+                        lhsT_scale=hq[nt][1][:, g, P * s:P * s + P],
                         rhs=w2c[:, g, :].bitcast(FP8X4),
                         rhs_scale=w2s[:, g, :],
                         start=(g == 0), stop=(g == 1),
                     )
+
+        def outx(nt):
             osb = work.tile([P, SUB, T], F32, tag="osb", bufs=3)
-            nc.vector.scalar_tensor_tensor(out=osb[:], in0=o[:], scalar=OUT_SCALE,
+            nc.vector.scalar_tensor_tensor(out=osb[:], in0=oo[nt][:], scalar=OUT_SCALE,
                                            in1=b2s[:].unsqueeze(1).to_broadcast([P, SUB, T]),
                                            op0=ALU.mult, op1=ALU.add)
             nc.sync.dma_start(out=outv[nt], in_=osb[:].rearrange("p s t -> p (s t)"))
 
-        features(0)
-        weights()
-        features(1)
-        prev = None
-        for nt in range(NT):
-            if nt + 2 < NT:
-                features(nt + 2)
-            cur = stage1(nt)
-            if prev is not None:
-                stage2(nt - 1, prev[0], prev[1])
-            prev = cur
-        stage2(NT - 1, prev[0], prev[1])
+        for c in range(TH_LEAD):
+            theta(c)
+        for tau in range(NCH + MLP_LAG + 7):
+            u = tau - MLP_LAG
+            if tau + TH_LEAD < NCH:
+                theta(tau + TH_LEAD)
+            w_units = [k for k in range(W_PER_SLOT * (tau - W_SLOT0), W_PER_SLOT * (tau - W_SLOT0 + 1)) if 0 <= k < 16]
+            for k in w_units:
+                w1_pe(k)
+            if u - 5 >= 0 and (u - 5) % 4 == 0 and (u - 5) // 4 < NT:
+                mm2((u - 5) // 4)
+            if 0 <= u < NCH:
+                mm1(u // 4, 2 * (u % 4))
+                mm1(u // 4, 2 * (u % 4) + 1)
+            if u - 2 >= 0 and (u - 2) % 4 == 0 and (u - 2) // 4 < NT:
+                regroup((u - 2) // 4, 0)
+            if u - 4 >= 0 and (u - 4) % 4 == 0 and (u - 4) // 4 < NT:
+                regroup((u - 4) // 4, 1)
+            if 0 <= u < NCH:
+                silu(u // 4, 2 * (u % 4))
+            if tau < NCH:
+                reduce(tau)
+            if 0 <= tau - 1 < NCH:
+                sin_s(tau - 1)
+            for k in w_units:
+                w1_exit(k)
+            if 0 <= u < NCH:
+                silu(u // 4, 2 * (u % 4) + 1)
+            if 0 <= tau - 1 < NCH:
+                fold(tau - 1)
+            if 0 <= tau - 2 < NCH:
+                sin_c(tau - 2)
+            if tau - 5 >= 0 and (tau - 5) % 4 == 0 and (tau - 5) // 4 < NT:
+                quant_f((tau - 5) // 4, 0)
+            if tau - 6 >= 0 and (tau - 6) % 4 == 0 and (tau - 6) // 4 < NT:
+                quant_f((tau - 6) // 4, 1)
+            for k in w_units:
+                w1_quant(k)
+            if tau == W_SLOT0 + 16 // W_PER_SLOT:
+                small_weights()
+            if u - 2 >= 0 and (u - 2) % 4 == 0 and (u - 2) // 4 < NT:
+                quant_h((u - 2) // 4, 0)
+            if u - 4 >= 0 and (u - 4) % 4 == 0 and (u - 4) // 4 < NT:
+                quant_h((u - 4) // 4, 1)
+            if u - 6 >= 0 and (u - 6) % 4 == 0 and (u - 6) // 4 < NT:
+                outx((u - 6) // 4)

@@ -28,7 +28,7 @@ TWO_PI = 2.0 * math.pi
 OUT_SCALE = 1.0 / math.sqrt(128.0)
 
 PIN = False
-ABS_DVE_EVERY = 3
+ABS_DVE_EVERY = 2
 TH_BUFS = 3
 Z_BUFS = 4
 O_BUFS = 1
@@ -220,15 +220,22 @@ def tile_gabtemplatemlp_t_kernel(tc, seq_len, freqs, W1, b1, W2, b2, dr, dc, out
 
         def silu(nt, j):
             if j == 0:
-                hpl[nt] = work.tile([P, MT, 512], BF16, tag="hpl", bufs=2, name="hpl")
+                hpl[nt] = work.tile([P, MT, 512], BF16, tag="hpl", bufs=3, name="hpl")
             nc.scalar.activation(out=hpl[nt][:, j, :], in_=zz[(nt, j)][:], func=ACT.Silu, bias=b1c[:, j:j + 1])
 
         def regroup(nt, g):
-            hgr[(nt, g)] = work.tile([P, 512, 4], BF16, tag="hg", bufs=3, align_bytes=64, name="hg")
-            nc.vector.tensor_copy(
-                out=hgr[(nt, g)][:].rearrange("p (c i) t -> p c t i", i=4),
-                in_=hpl[nt][:, 4 * g:4 * g + 4, :].rearrange("p t (c i) -> p c t i", i=4),
-            )
+            hgr[(nt, g)] = work.tile([P, 512, 4], BF16, tag="hg", bufs=4, align_bytes=64, name="hg")
+            if g == 1 and nt < NT - 1:
+                for half in range(2):
+                    cols = slice(half * (512 // 2), (half + 1) * (512 // 2))
+                    nc.gpsimd.tensor_scalar(out=hgr[(nt, g)][:, cols, :],
+                                            in0=hpl[nt][:, 4 * g:4 * g + 4, cols].rearrange("p t n -> p n t"),
+                                            scalar1=1.0, scalar2=0.0, op0=ALU.mult, op1=ALU.add)
+            else:
+                nc.vector.tensor_copy(
+                    out=hgr[(nt, g)][:].rearrange("p (c i) t -> p c t i", i=4),
+                    in_=hpl[nt][:, 4 * g:4 * g + 4, :].rearrange("p t (c i) -> p c t i", i=4),
+                )
 
         def quant_h(nt, g):
             if g == 0:

@@ -28,7 +28,7 @@ TWO_PI = 2.0 * math.pi
 OUT_SCALE = 1.0 / math.sqrt(128.0)
 
 PIN = False
-ABS_DVE_EVERY = 2
+ABS_DVE_EVERY = 1000
 TH_BUFS = 3
 Z_BUFS = 4
 O_BUFS = 1
@@ -220,22 +220,15 @@ def tile_gabtemplatemlp_t_kernel(tc, seq_len, freqs, W1, b1, W2, b2, dr, dc, out
 
         def silu(nt, j):
             if j == 0:
-                hpl[nt] = work.tile([P, MT, 512], BF16, tag="hpl", bufs=3, name="hpl")
+                hpl[nt] = work.tile([P, MT, 512], BF16, tag="hpl", bufs=2, name="hpl")
             nc.scalar.activation(out=hpl[nt][:, j, :], in_=zz[(nt, j)][:], func=ACT.Silu, bias=b1c[:, j:j + 1])
 
         def regroup(nt, g):
-            hgr[(nt, g)] = work.tile([P, 512, 4], BF16, tag="hg", bufs=4, align_bytes=64, name="hg")
-            if g == 1 and nt < NT - 1:
-                for half in range(2):
-                    cols = slice(half * (512 // 2), (half + 1) * (512 // 2))
-                    nc.gpsimd.tensor_scalar(out=hgr[(nt, g)][:, cols, :],
-                                            in0=hpl[nt][:, 4 * g:4 * g + 4, cols].rearrange("p t n -> p n t"),
-                                            scalar1=1.0, scalar2=0.0, op0=ALU.mult, op1=ALU.add)
-            else:
-                nc.vector.tensor_copy(
-                    out=hgr[(nt, g)][:].rearrange("p (c i) t -> p c t i", i=4),
-                    in_=hpl[nt][:, 4 * g:4 * g + 4, :].rearrange("p t (c i) -> p c t i", i=4),
-                )
+            hgr[(nt, g)] = work.tile([P, 512, 4], BF16, tag="hg", bufs=3, align_bytes=64, name="hg")
+            nc.vector.tensor_copy(
+                out=hgr[(nt, g)][:].rearrange("p (c i) t -> p c t i", i=4),
+                in_=hpl[nt][:, 4 * g:4 * g + 4, :].rearrange("p t (c i) -> p c t i", i=4),
+            )
 
         def quant_h(nt, g):
             if g == 0:

@@ -28,7 +28,7 @@ TWO_PI = 2.0 * math.pi
 OUT_SCALE = 1.0 / math.sqrt(128.0)
 
 PIN = False
-ABS_DVE_EVERY = 1000
+ABS_DVE_EVERY = 2
 TH_BUFS = 3
 Z_BUFS = 4
 O_BUFS = 1

@@ -88,28 +88,28 @@ def tile_gabtemplatemlp_t_kernel(tc, seq_len, freqs, W1, b1, W2, b2, dr, dc, out
         xmov = const.tile([P, SUB, P, 4], BF16)
         ddv = dd[:].rearrange("k (n s) -> k s n", s=SUB)
 
-        def build_x(s):
-            nc.vector.tensor_tensor(
+        def build_x(eng, s):
+            eng.tensor_tensor(
                 out=xmov[:, s, :, :],
                 in0=ddv[:, s, :].unsqueeze(2).to_broadcast([P, P, 4]),
                 in1=coef[:].unsqueeze(1).to_broadcast([P, P, 4]),
                 op=ALU.mult,
             )
 
-        def build_l(lo, hi):
-            nc.vector.tensor_tensor(
+        def build_l(eng, lo, hi):
+            eng.tensor_tensor(
                 out=lsel[:, lo:hi, :],
                 in0=fb[:].unsqueeze(1).to_broadcast([P, hi - lo, P]),
                 in1=mask[:, lo:hi].unsqueeze(2).to_broadcast([P, hi - lo, P]),
                 op=ALU.mult,
             )
 
-        build_x(0)
-        build_l(0, 1)
-        build_x(1)
-        build_x(2)
-        build_x(3)
-        build_l(1, NT)
+        build_x(nc.vector, 0)
+        build_l(nc.vector, 0, 1)
+        build_x(nc.gpsimd, 1)
+        build_x(nc.gpsimd, 2)
+        build_x(nc.gpsimd, 3)
+        build_l(nc.gpsimd, 1, NT)
 
         fcodes = const.tile([P, 2, NT, 512], U32, align_bytes=64)
         fscales = const.tile([P, 2, NT, 512], U8, align_bytes=64)
@@ -140,7 +140,7 @@ def tile_gabtemplatemlp_t_kernel(tc, seq_len, freqs, W1, b1, W2, b2, dr, dc, out
         def reduce(c):
             kk = work.tile([P, 512], I32, tag="kk", bufs=3)
             nc.vector.tensor_scalar(out=kk[:], in0=th[c][:], scalar1=INV_2PI, scalar2=None, op0=ALU.mult)
-            rr[c] = work.tile([P, 512], F32, tag="r", bufs=4, name="r")
+            rr[c] = work.tile([P, 512], F32, tag="r", bufs=6, name="r")
             nc.vector.scalar_tensor_tensor(out=rr[c][:], in0=th[c][:], scalar=INV_2PI, in1=kk[:],
                                            op0=ALU.mult, op1=ALU.subtract)
 
@@ -151,10 +151,10 @@ def tile_gabtemplatemlp_t_kernel(tc, seq_len, freqs, W1, b1, W2, b2, dr, dc, out
             nc.scalar.activation(out=feat[(nt, 0)][:, 512 * s:512 * s + 512], in_=rr[c][:], func=ACT.Sin, scale=TWO_PI)
 
         def abs_on_dve(c):
-            return c % ABS_DVE_EVERY == ABS_DVE_EVERY - 1
+            return c >= 0 and c % 2 < 1
 
         def fold(c):
-            ab[c] = work.tile([P, 512], F32, tag="ab", bufs=4, name="ab")
+            ab[c] = work.tile([P, 512], F32, tag="ab", bufs=6, name="ab")
             if abs_on_dve(c):
                 nc.vector.scalar_tensor_tensor(out=ab[c][:], in0=rr[c][:], scalar=-1.0, in1=rr[c][:],
                                                op0=ALU.mult, op1=ALU.max)
@@ -220,11 +220,11 @@ def tile_gabtemplatemlp_t_kernel(tc, seq_len, freqs, W1, b1, W2, b2, dr, dc, out
 
         def silu(nt, j):
             if j == 0:
-                hpl[nt] = work.tile([P, MT, 512], BF16, tag="hpl", bufs=2, name="hpl")
+                hpl[nt] = work.tile([P, MT, 512], BF16, tag="hpl", bufs=3, name="hpl")
             nc.scalar.activation(out=hpl[nt][:, j, :], in_=zz[(nt, j)][:], func=ACT.Silu, bias=b1c[:, j:j + 1])
 
         def regroup(nt, g):
-            hgr[(nt, g)] = work.tile([P, 512, 4], BF16, tag="hg", bufs=3, align_bytes=64, name="hg")
+            hgr[(nt, g)] = work.tile([P, 512, 4], BF16, tag="hg", bufs=4, align_bytes=64, name="hg")
             nc.vector.tensor_copy(
                 out=hgr[(nt, g)][:].rearrange("p (c i) t -> p c t i", i=4),
                 in_=hpl[nt][:, 4 * g:4 * g + 4, :].rearrange("p t (c i) -> p c t i", i=4),

@@ -82,34 +82,30 @@ def tile_gabtemplatemlp_t_kernel(tc, seq_len, freqs, W1, b1, W2, b2, dr, dc, out
         nc.vector.memset(coef[0:32, 2:4], 1.0)
         nc.vector.memset(coef[32:64, 1:3], 1.0)
         nc.vector.memset(coef[32:64, 3:4], -1.0)
-        mask = const.tile([P, NT], BF16)
+        mask = const.tile([P, NT], F32)
         nc.vector.tensor_tensor(out=mask[:], in0=ident[:, 0:NT], in1=ident[:, 32:32 + NT], op=ALU.add)
         lsel = const.tile([P, NT, P], BF16)
         xmov = const.tile([P, SUB, P, 4], BF16)
         ddv = dd[:].rearrange("k (n s) -> k s n", s=SUB)
 
-        def build_x(eng, s):
-            eng.tensor_tensor(
+        def build_x(s):
+            nc.vector.tensor_tensor(
                 out=xmov[:, s, :, :],
                 in0=ddv[:, s, :].unsqueeze(2).to_broadcast([P, P, 4]),
                 in1=coef[:].unsqueeze(1).to_broadcast([P, P, 4]),
                 op=ALU.mult,
             )
 
-        def build_l(eng, lo, hi):
-            eng.tensor_tensor(
-                out=lsel[:, lo:hi, :],
-                in0=fb[:].unsqueeze(1).to_broadcast([P, hi - lo, P]),
-                in1=mask[:, lo:hi].unsqueeze(2).to_broadcast([P, hi - lo, P]),
-                op=ALU.mult,
-            )
+        def build_l(lo, hi):
+            for a in range(lo, hi):
+                nc.scalar.activation(out=lsel[:, a, :], in_=fb[:], func=ACT.Copy, scale=mask[:, a:a + 1])
 
-        build_x(nc.vector, 0)
-        build_l(nc.vector, 0, 1)
-        build_x(nc.gpsimd, 1)
-        build_x(nc.gpsimd, 2)
-        build_x(nc.gpsimd, 3)
-        build_l(nc.gpsimd, 1, NT)
+        build_x(0)
+        build_l(0, 1)
+        build_x(1)
+        build_x(2)
+        build_x(3)
+        build_l(1, NT)
 
         fcodes = const.tile([P, 2, NT, 512], U32, align_bytes=64)
         fscales = const.tile([P, 2, NT, 512], U8, align_bytes=64)
@@ -140,7 +136,7 @@ def tile_gabtemplatemlp_t_kernel(tc, seq_len, freqs, W1, b1, W2, b2, dr, dc, out
         def reduce(c):
             kk = work.tile([P, 512], I32, tag="kk", bufs=3)
             nc.vector.tensor_scalar(out=kk[:], in0=th[c][:], scalar1=INV_2PI, scalar2=None, op0=ALU.mult)
-            rr[c] = work.tile([P, 512], F32, tag="r", bufs=6, name="r")
+            rr[c] = work.tile([P, 512], F32, tag="r", bufs=4, name="r")
             nc.vector.scalar_tensor_tensor(out=rr[c][:], in0=th[c][:], scalar=INV_2PI, in1=kk[:],
                                            op0=ALU.mult, op1=ALU.subtract)
 
@@ -151,10 +147,10 @@ def tile_gabtemplatemlp_t_kernel(tc, seq_len, freqs, W1, b1, W2, b2, dr, dc, out
             nc.scalar.activation(out=feat[(nt, 0)][:, 512 * s:512 * s + 512], in_=rr[c][:], func=ACT.Sin, scale=TWO_PI)
 
         def abs_on_dve(c):
-            return c >= 0 and c % 2 < 1
+            return c % ABS_DVE_EVERY == ABS_DVE_EVERY - 1
 
         def fold(c):
-            ab[c] = work.tile([P, 512], F32, tag="ab", bufs=6, name="ab")
+            ab[c] = work.tile([P, 512], F32, tag="ab", bufs=4, name="ab")
             if abs_on_dve(c):
                 nc.vector.scalar_tensor_tensor(out=ab[c][:], in0=rr[c][:], scalar=-1.0, in1=rr[c][:],
                                                op0=ALU.mult, op1=ALU.max)
@@ -220,22 +216,29 @@ def tile_gabtemplatemlp_t_kernel(tc, seq_len, freqs, W1, b1, W2, b2, dr, dc, out
 
         def silu(nt, j):
             if j == 0:
-                hpl[nt] = work.tile([P, MT, 512], BF16, tag="hpl", bufs=3, name="hpl")
+                hpl[nt] = work.tile([P, MT, 512], BF16, tag="hpl", bufs=2, name="hpl")
             nc.scalar.activation(out=hpl[nt][:, j, :], in_=zz[(nt, j)][:], func=ACT.Silu, bias=b1c[:, j:j + 1])
 
+        def pieces(nt, g):
+            if nt == NT - 1 and g == 1:
+                return [(0, 256), (256, 512)]
+            return [(0, 512)]
+
         def regroup(nt, g):
-            hgr[(nt, g)] = work.tile([P, 512, 4], BF16, tag="hg", bufs=4, align_bytes=64, name="hg")
-            nc.vector.tensor_copy(
-                out=hgr[(nt, g)][:].rearrange("p (c i) t -> p c t i", i=4),
-                in_=hpl[nt][:, 4 * g:4 * g + 4, :].rearrange("p t (c i) -> p c t i", i=4),
-            )
+            hgr[(nt, g)] = work.tile([P, 512, 4], BF16, tag="hg", bufs=3, align_bytes=64, name="hg")
+            for lo, hi in pieces(nt, g):
+                nc.vector.tensor_copy(
+                    out=hgr[(nt, g)][:, lo:hi, :].rearrange("p (c i) t -> p c t i", i=4),
+                    in_=hpl[nt][:, 4 * g:4 * g + 4, lo:hi].rearrange("p t (c i) -> p c t i", i=4),
+                )
 
         def quant_h(nt, g):
             if g == 0:
                 hq[nt] = (work.tile([P, 2, 512], U32, tag="hc", bufs=2, align_bytes=64, name="hc"),
                           work.tile([P, 2, 512], U8, tag="hs", bufs=2, align_bytes=64, name="hs"))
-            nc.vector.quantize_mx(out=hq[nt][0][:, g, :].bitcast(FP8X4), scales=hq[nt][1][:, g, :],
-                                  in_=hgr[(nt, g)][:].rearrange("p w t -> p (w t)"))
+            for lo, hi in pieces(nt, g):
+                nc.vector.quantize_mx(out=hq[nt][0][:, g, lo:hi].bitcast(FP8X4), scales=hq[nt][1][:, g, lo:hi],
+                                      in_=hgr[(nt, g)][:, lo:hi, :].rearrange("p w t -> p (w t)"))
 
         def mm2(nt):
             oo[nt] = ps_o.tile([P, SUB, T], F32, tag="o", name="o")
@@ -252,10 +255,12 @@ def tile_gabtemplatemlp_t_kernel(tc, seq_len, freqs, W1, b1, W2, b2, dr, dc, out
 
         def outx(nt):
             osb = work.tile([P, SUB, T], F32, tag="osb", bufs=3)
-            nc.vector.scalar_tensor_tensor(out=osb[:], in0=oo[nt][:], scalar=OUT_SCALE,
-                                           in1=b2s[:].unsqueeze(1).to_broadcast([P, SUB, T]),
-                                           op0=ALU.mult, op1=ALU.add)
-            nc.sync.dma_start(out=outv[nt], in_=osb[:].rearrange("p s t -> p (s t)"))
+            for lo, hi in pieces(nt, 1):
+                a, b = lo // P, hi // P
+                nc.vector.scalar_tensor_tensor(out=osb[:, a:b, :], in0=oo[nt][:, a:b, :], scalar=OUT_SCALE,
+                                               in1=b2s[:].unsqueeze(1).to_broadcast([P, b - a, T]),
+                                               op0=ALU.mult, op1=ALU.add)
+                nc.sync.dma_start(out=outv[nt][:, T * a:T * b], in_=osb[:, a:b, :].rearrange("p s t -> p (s t)"))
 
         for c in range(TH_LEAD):
             theta(c)

@@ -119,6 +119,7 @@ def tile_gabtemplatemlp_t_kernel(tc, seq_len, freqs, W1, b1, W2, b2, dr, dc, out
 
         th = {}
         rr = {}
+        kk = {}
         ab = {}
         feat = {}
         zz = {}
@@ -133,11 +134,13 @@ def tile_gabtemplatemlp_t_kernel(tc, seq_len, freqs, W1, b1, W2, b2, dr, dc, out
             nc.tensor.matmul(out=th[c][:], lhsT=lsel[:, c // SUB, :],
                              rhs=xmov[:, c % SUB, :, :].rearrange("k n t -> k (n t)"), start=True, stop=True)
 
+        def turns(c):
+            kk[c] = work.tile([P, 512], I32, tag="kk", bufs=3, name="kk")
+            nc.vector.tensor_scalar(out=kk[c][:], in0=th[c][:], scalar1=INV_2PI, scalar2=None, op0=ALU.mult)
+
         def reduce(c):
-            kk = work.tile([P, 512], I32, tag="kk", bufs=3)
-            nc.vector.tensor_scalar(out=kk[:], in0=th[c][:], scalar1=INV_2PI, scalar2=None, op0=ALU.mult)
             rr[c] = work.tile([P, 512], F32, tag="r", bufs=4, name="r")
-            nc.vector.scalar_tensor_tensor(out=rr[c][:], in0=th[c][:], scalar=INV_2PI, in1=kk[:],
+            nc.vector.scalar_tensor_tensor(out=rr[c][:], in0=th[c][:], scalar=INV_2PI, in1=kk[c][:],
                                            op0=ALU.mult, op1=ALU.subtract)
 
         def sin_s(c):
@@ -264,6 +267,7 @@ def tile_gabtemplatemlp_t_kernel(tc, seq_len, freqs, W1, b1, W2, b2, dr, dc, out
 
         for c in range(TH_LEAD):
             theta(c)
+        turns(0)
         for tau in range(NCH + MLP_LAG + 7):
             u = tau - MLP_LAG
             if tau + TH_LEAD < NCH:
@@ -282,6 +286,8 @@ def tile_gabtemplatemlp_t_kernel(tc, seq_len, freqs, W1, b1, W2, b2, dr, dc, out
                 regroup((u - 4) // 4, 1)
             if 0 <= u < NCH:
                 silu(u // 4, 2 * (u % 4))
+            if tau + 1 < NCH:
+                turns(tau + 1)
             if tau < NCH:
                 reduce(tau)
             if 0 <= tau - 1 < NCH:

@@ -27,45 +27,69 @@ INV_2PI = 1.0 / (2.0 * math.pi)
 TWO_PI = 2.0 * math.pi
 OUT_SCALE = 1.0 / math.sqrt(128.0)
 
-PIN = False
-ABS_DVE_EVERY = 2
-TH_BUFS = 3
-Z_BUFS = 4
+ABS_ON_SCALAR = (1, 5)
+Z_BUFS = 7
 O_BUFS = 1
-TH_LEAD = 2
-W_SLOT0 = 2
-W_PER_SLOT = 4
-MLP_LAG = 7
+MLP_LAG = 9
+RG_LAG = (3, 5)
+QH_LAG = (4, 6)
+MM2_LAG = 7
+OUT_LAG = 8
+QF_LAG = (5, 6)
+PARK = PAIRS - P
 
 
 def tile_gabtemplatemlp_t_kernel(tc, seq_len, freqs, W1, b1, W2, b2, dr, dc, out):
     nc = tc.nc
     with ExitStack() as ctx:
-        if PIN:
-            ctx.enter_context(tc.manual_schedule())
+        ctx.enter_context(tc.manual_schedule())
         const = ctx.enter_context(tc.tile_pool(name="const", bufs=1))
         work = ctx.enter_context(tc.tile_pool(name="work", bufs=2))
-        ps_th = ctx.enter_context(tc.psum_pool(name="ps_th", bufs=TH_BUFS))
         ps_z = ctx.enter_context(tc.psum_pool(name="ps_z", bufs=Z_BUFS))
         ps_o = ctx.enter_context(tc.psum_pool(name="ps_o", bufs=O_BUFS))
 
-        dd = const.tile([P, 512], BF16)
-        nc.vector.memset(dd[:], 0.0)
-        nc.sync.dma_start(out=dd[0:8, :], in_=dr.rearrange("i j -> (i j)").rearrange("(a n) -> a n", n=512))
-        nc.sync.dma_start(out=dd[32:40, :], in_=dc.rearrange("i j -> (i j)").rearrange("(a n) -> a n", n=512))
-        fb = const.tile([P, P], BF16)
-        nc.sync.dma_start(out=fb[:], in_=freqs.partition_broadcast(P))
-        w1raw = const.tile([P, 32, 256], BF16)
-        w1v = W1.rearrange("h f -> (h f)").rearrange("(b q x) -> q b x", q=P, x=256)
-        for part in range(4):
-            nc.sync.dma_start(out=w1raw[:, 8 * part:8 * part + 8, :], in_=w1v[:, 8 * part:8 * part + 8, :])
+        drc = const.tile([P, 32], BF16)
+        nc.sync.dma_start(out=drc[:], in_=dr.rearrange("i j -> (i j)").rearrange("(q n) -> q n", n=32))
+        dcc = const.tile([P, 32], BF16)
+        nc.sync.dma_start(out=dcc[:], in_=dc.rearrange("i j -> (i j)").rearrange("(q n) -> q n", n=32))
         brow = const.tile([P, P], BF16)
         nc.vector.memset(brow[:], 0.0)
         nc.sync.dma_start(out=brow[0:8, :], in_=b1.rearrange("(j p) -> j p", p=P))
+        nc.sync.dma_start(out=brow[8:9, :], in_=freqs.rearrange("(o p) -> o p", o=1))
+        w1raw = const.tile([P, 32, 256], BF16)
+        w1v = W1.rearrange("h f -> (h f)").rearrange("(b q x) -> q b x", q=P, x=256)
+
+        def load_w1(part):
+            nc.sync.dma_start(out=w1raw[:, 8 * part:8 * part + 8, :], in_=w1v[:, 8 * part:8 * part + 8, :])
+
+        load_w1(0)
+
+        x4 = const.tile([P, 32, 4], F32)
+        nc.vector.tensor_copy(out=x4[:, :, 0], in_=drc[:])
+        nc.vector.tensor_copy(out=x4[:, :, 1], in_=dcc[:])
+        nc.vector.tensor_tensor(out=x4[:, :, 2], in0=drc[:], in1=dcc[:], op=ALU.add)
+        nc.vector.tensor_tensor(out=x4[:, :, 3], in0=drc[:], in1=dcc[:], op=ALU.subtract)
+        rows = out.rearrange("i j t -> (i j) t")
+        nc.sync.dma_start(out=rows[PARK:PAIRS, :], in_=x4[:].rearrange("q n t -> q (n t)"))
+        parked = rows[PARK:PAIRS, :].rearrange("q x -> (q x)")
+        xs = const.tile([P, NT, 2048], F32)
+
+        def load_x(a, lo, hi):
+            nc.sync.dma_start(out=xs[:, a, lo:hi], in_=parked[2048 * a + lo:2048 * a + hi].partition_broadcast(P))
+
+        load_w1(1)
+        load_w1(2)
+        load_x(0, 0, 512)
+        load_x(0, 512, 1024)
+        load_w1(3)
+        load_x(0, 1024, 2048)
         w2raw = const.tile([P, HID], BF16)
         nc.sync.dma_start(out=w2raw[:], in_=W2)
+        load_x(1, 0, 2048)
         b2b = const.tile([P, T], BF16)
         nc.sync.dma_start(out=b2b[:], in_=b2.partition_broadcast(P))
+        for a in range(2, NT):
+            load_x(a, 0, 2048)
 
         warm = const.tile([P, 1], F32)
         nc.vector.memset(warm[:], 0.0)
@@ -76,50 +100,19 @@ def tile_gabtemplatemlp_t_kernel(tc, seq_len, freqs, W1, b1, W2, b2, dr, dc, out
         nc.vector.memset(one[:], 1.0)
         halfpi = const.tile([P, 1], F32)
         nc.vector.tensor_scalar(out=halfpi[:], in0=one[:], scalar1=math.pi / 2.0, scalar2=None, op0=ALU.mult)
-        coef = const.tile([P, 4], BF16)
-        nc.vector.memset(coef[:], 0.0)
-        nc.vector.memset(coef[0:32, 0:1], 1.0)
-        nc.vector.memset(coef[0:32, 2:4], 1.0)
-        nc.vector.memset(coef[32:64, 1:3], 1.0)
-        nc.vector.memset(coef[32:64, 3:4], -1.0)
-        mask = const.tile([P, NT], F32)
-        nc.vector.tensor_tensor(out=mask[:], in0=ident[:, 0:NT], in1=ident[:, 32:32 + NT], op=ALU.add)
-        lsel = const.tile([P, NT, P], BF16)
-        xmov = const.tile([P, SUB, P, 4], BF16)
-        ddv = dd[:].rearrange("k (n s) -> k s n", s=SUB)
 
-        def build_x(s):
-            nc.vector.tensor_tensor(
-                out=xmov[:, s, :, :],
-                in0=ddv[:, s, :].unsqueeze(2).to_broadcast([P, P, 4]),
-                in1=coef[:].unsqueeze(1).to_broadcast([P, P, 4]),
-                op=ALU.mult,
-            )
-
-        def build_l(lo, hi):
-            for a in range(lo, hi):
-                nc.scalar.activation(out=lsel[:, a, :], in_=fb[:], func=ACT.Copy, scale=mask[:, a:a + 1])
-
-        build_x(0)
-        build_l(0, 1)
-        build_x(1)
-        build_x(2)
-        build_x(3)
-        build_l(1, NT)
-
-        fcodes = const.tile([P, 2, NT, 512], U32, align_bytes=64)
-        fscales = const.tile([P, 2, NT, 512], U8, align_bytes=64)
         w1c = const.tile([P, 2, HID], U32, align_bytes=64)
         w1s = const.tile([P, 2, HID], U8, align_bytes=64)
         w2c = const.tile([P, 2, T], U32, align_bytes=64)
         w2s = const.tile([P, 2, T], U8, align_bytes=64)
         b1c = const.tile([P, MT], F32)
+        fcol = const.tile([P, 1], F32)
         b2s = const.tile([P, T], F32)
-        outv = out.rearrange("i j t -> (i j) t").rearrange("(a n s) t -> a n (s t)", n=P, s=SUB)
+        outv = rows.rearrange("(a s n) t -> a n s t", n=P, s=SUB)
 
-        th = {}
-        rr = {}
         kk = {}
+        rr = {}
+        fq = {}
         ab = {}
         feat = {}
         zz = {}
@@ -129,46 +122,47 @@ def tile_gabtemplatemlp_t_kernel(tc, seq_len, freqs, W1, b1, W2, b2, dr, dc, out
         oo = {}
         wts = {}
 
-        def theta(c):
-            th[c] = ps_th.tile([P, 512], F32, tag="th", name="th")
-            nc.tensor.matmul(out=th[c][:], lhsT=lsel[:, c // SUB, :],
-                             rhs=xmov[:, c % SUB, :, :].rearrange("k n t -> k (n t)"), start=True, stop=True)
+        pieces_f = [(0, 512 * s, 512) for s in range(4)] + [(nt, 1024 * h, 1024) for nt in range(1, NT) for h in range(2)]
+        slot_f = {4 * nt + lo // 512: i for i, (nt, lo, n) in enumerate(pieces_f)}
 
-        def turns(c):
-            kk[c] = work.tile([P, 512], I32, tag="kk", bufs=3, name="kk")
-            nc.vector.tensor_scalar(out=kk[c][:], in0=th[c][:], scalar1=INV_2PI, scalar2=None, op0=ALU.mult)
+        def turns(i):
+            nt, lo, n = pieces_f[i]
+            kk[i] = work.tile([P, n], I32, tag="kk", bufs=3, name="kk")
+            nc.vector.tensor_scalar(out=kk[i][:], in0=xs[:, nt, lo:lo + n], scalar1=fcol[:, 0:1], scalar2=None, op0=ALU.mult)
 
-        def reduce(c):
-            rr[c] = work.tile([P, 512], F32, tag="r", bufs=4, name="r")
-            nc.vector.scalar_tensor_tensor(out=rr[c][:], in0=th[c][:], scalar=INV_2PI, in1=kk[c][:],
+        def reduce(i):
+            nt, lo, n = pieces_f[i]
+            rr[i] = work.tile([P, n], F32, tag="r", bufs=3, name="r")
+            nc.vector.scalar_tensor_tensor(out=rr[i][:], in0=xs[:, nt, lo:lo + n], scalar=fcol[:, 0:1], in1=kk[i][:],
                                            op0=ALU.mult, op1=ALU.subtract)
 
-        def sin_s(c):
-            nt, s = c // SUB, c % SUB
-            if s == 0:
-                feat[(nt, 0)] = work.tile([P, 2048], BF16, tag="fs", bufs=3, align_bytes=64, name="fs")
-            nc.scalar.activation(out=feat[(nt, 0)][:, 512 * s:512 * s + 512], in_=rr[c][:], func=ACT.Sin, scale=TWO_PI)
+        def sin_s(i):
+            nt, lo, n = pieces_f[i]
+            if lo == 0:
+                feat[(nt, 0)] = work.tile([P, 2048], BF16, tag="fs", bufs=2, align_bytes=64, name="fs")
+            nc.scalar.activation(out=feat[(nt, 0)][:, lo:lo + n], in_=rr[i][:], func=ACT.Sin, scale=TWO_PI)
 
-        def abs_on_dve(c):
-            return c % ABS_DVE_EVERY == ABS_DVE_EVERY - 1
-
-        def fold(c):
-            ab[c] = work.tile([P, 512], F32, tag="ab", bufs=4, name="ab")
-            if abs_on_dve(c):
-                nc.vector.scalar_tensor_tensor(out=ab[c][:], in0=rr[c][:], scalar=-1.0, in1=rr[c][:],
-                                               op0=ALU.mult, op1=ALU.max)
+        def fold(i):
+            nt, lo, n = pieces_f[i]
+            ab[i] = work.tile([P, n], F32, tag="ab", bufs=3, name="ab")
+            if i % 8 in ABS_ON_SCALAR:
+                nc.scalar.activation(out=ab[i][:], in_=rr[i][:], func=ACT.Abs)
             else:
-                nc.scalar.activation(out=ab[c][:], in_=rr[c][:], func=ACT.Abs)
+                nc.vector.scalar_tensor_tensor(out=ab[i][:], in0=rr[i][:], scalar=-1.0, in1=rr[i][:],
+                                               op0=ALU.mult, op1=ALU.max)
 
-        def sin_c(c):
-            nt, s = c // SUB, c % SUB
-            if s == 0:
-                feat[(nt, 1)] = work.tile([P, 2048], BF16, tag="fc", bufs=3, align_bytes=64, name="fc")
-            nc.scalar.activation(out=feat[(nt, 1)][:, 512 * s:512 * s + 512], in_=ab[c][:], func=ACT.Sin,
+        def sin_c(i):
+            nt, lo, n = pieces_f[i]
+            if lo == 0:
+                feat[(nt, 1)] = work.tile([P, 2048], BF16, tag="fc", bufs=2, align_bytes=64, name="fc")
+            nc.scalar.activation(out=feat[(nt, 1)][:, lo:lo + n], in_=ab[i][:], func=ACT.Sin,
                                  scale=-TWO_PI, bias=halfpi[:])
 
         def quant_f(nt, sp):
-            nc.vector.quantize_mx(out=fcodes[:, sp, nt, :].bitcast(FP8X4), scales=fscales[:, sp, nt, :],
+            if sp == 0:
+                fq[nt] = (work.tile([P, 2, 512], U32, tag="fqc", bufs=3, align_bytes=64, name="fqc"),
+                          work.tile([P, 2, 512], U8, tag="fqs", bufs=3, align_bytes=64, name="fqs"))
+            nc.vector.quantize_mx(out=fq[nt][0][:, sp, :].bitcast(FP8X4), scales=fq[nt][1][:, sp, :],
                                   in_=feat[(nt, sp)][:])
 
         def w1_pe(u):
@@ -180,7 +174,10 @@ def tile_gabtemplatemlp_t_kernel(tc, seq_len, freqs, W1, b1, W2, b2, dr, dc, out
 
         def w1_exit(u):
             wg = work.tile([P, 512], BF16, tag="wg", bufs=4, align_bytes=64)
-            nc.scalar.copy(out=wg[:], in_=wts[u][:])
+            if u % 2 == 0:
+                nc.scalar.copy(out=wg[:], in_=wts[u][:])
+            else:
+                nc.vector.tensor_copy(out=wg[:], in_=wts[u][:])
             wts[u] = wg
 
         def w1_quant(u):
@@ -188,10 +185,13 @@ def tile_gabtemplatemlp_t_kernel(tc, seq_len, freqs, W1, b1, W2, b2, dr, dc, out
             nc.vector.quantize_mx(out=w1c[:, sp, P * j:P * j + P].bitcast(FP8X4),
                                   scales=w1s[:, sp, P * j:P * j + P], in_=wts[u][:])
 
-        def small_weights():
+        def columns():
             bt = ps_z.tile([P, P], BF16, tag="z")
             nc.tensor.transpose(out=bt[:], in_=brow[:], identity=ident[:])
+            nc.vector.tensor_scalar(out=fcol[:], in0=bt[:, MT:MT + 1], scalar1=INV_2PI, scalar2=None, op0=ALU.mult)
             nc.vector.tensor_copy(out=b1c[:], in_=bt[:, 0:MT])
+
+        def small_weights():
             nc.vector.tensor_scalar(out=b2s[:], in0=b2b[:], scalar1=OUT_SCALE, scalar2=None, op0=ALU.mult)
             w2g = {}
             for g in range(2):
@@ -212,8 +212,8 @@ def tile_gabtemplatemlp_t_kernel(tc, seq_len, freqs, W1, b1, W2, b2, dr, dc, out
                     out=zz[(nt, j)][:],
                     lhsT=w1c[:, sp, P * j:P * j + P].bitcast(FP8X4),
                     lhsT_scale=w1s[:, sp, P * j:P * j + P],
-                    rhs=fcodes[:, sp, nt, :].bitcast(FP8X4),
-                    rhs_scale=fscales[:, sp, nt, :],
+                    rhs=fq[nt][0][:, sp, :].bitcast(FP8X4),
+                    rhs_scale=fq[nt][1][:, sp, :],
                     start=(sp == 0), stop=(sp == 1),
                 )
 
@@ -263,54 +263,63 @@ def tile_gabtemplatemlp_t_kernel(tc, seq_len, freqs, W1, b1, W2, b2, dr, dc, out
                 nc.vector.scalar_tensor_tensor(out=osb[:, a:b, :], in0=oo[nt][:, a:b, :], scalar=OUT_SCALE,
                                                in1=b2s[:].unsqueeze(1).to_broadcast([P, b - a, T]),
                                                op0=ALU.mult, op1=ALU.add)
-                nc.sync.dma_start(out=outv[nt][:, T * a:T * b], in_=osb[:, a:b, :].rearrange("p s t -> p (s t)"))
+                nc.sync.dma_start(out=outv[nt][:, a:b, :], in_=osb[:, a:b, :])
 
-        for c in range(TH_LEAD):
-            theta(c)
-        turns(0)
-        for tau in range(NCH + MLP_LAG + 7):
-            u = tau - MLP_LAG
-            if tau + TH_LEAD < NCH:
-                theta(tau + TH_LEAD)
-            w_units = [k for k in range(W_PER_SLOT * (tau - W_SLOT0), W_PER_SLOT * (tau - W_SLOT0 + 1)) if 0 <= k < 16]
-            for k in w_units:
+        def w1_units(lo, hi):
+            for k in range(lo, hi):
                 w1_pe(k)
-            if u - 5 >= 0 and (u - 5) % 4 == 0 and (u - 5) // 4 < NT:
-                mm2((u - 5) // 4)
+                w1_exit(k)
+                if k >= 2:
+                    w1_quant(k - 2)
+
+        columns()
+        w1_units(0, 12)
+        turns(0)
+        for tau in range(NCH + MLP_LAG + OUT_LAG + 1):
+            u = tau - MLP_LAG
+
+            def tile_due(lag, t=tau):
+                return (t - lag) // 4 if (t - lag) >= 0 and (t - lag) % 4 == 0 and (t - lag) // 4 < NT else None
+
+            if 1 <= tau <= 2:
+                w1_units(10 + 2 * tau, 12 + 2 * tau)
+            if tau == 3:
+                w1_quant(14)
+                w1_quant(15)
+            if tau == 5:
+                small_weights()
             if 0 <= u < NCH:
                 mm1(u // 4, 2 * (u % 4))
                 mm1(u // 4, 2 * (u % 4) + 1)
-            if u - 2 >= 0 and (u - 2) % 4 == 0 and (u - 2) // 4 < NT:
-                regroup((u - 2) // 4, 0)
-            if u - 4 >= 0 and (u - 4) % 4 == 0 and (u - 4) // 4 < NT:
-                regroup((u - 4) // 4, 1)
+            nt = tile_due(MLP_LAG + MM2_LAG)
+            if nt is not None:
+                mm2(nt)
+            if tau in slot_f:
+                reduce(slot_f[tau])
+            for g in range(2):
+                nt = tile_due(MLP_LAG + RG_LAG[g])
+                if nt is not None:
+                    regroup(nt, g)
+            if tau in slot_f and slot_f[tau] + 1 < len(pieces_f):
+                turns(slot_f[tau] + 1)
             if 0 <= u < NCH:
                 silu(u // 4, 2 * (u % 4))
-            if tau + 1 < NCH:
-                turns(tau + 1)
-            if tau < NCH:
-                reduce(tau)
-            if 0 <= tau - 1 < NCH:
-                sin_s(tau - 1)
-            for k in w_units:
-                w1_exit(k)
+            if tau - 1 in slot_f:
+                sin_s(slot_f[tau - 1])
             if 0 <= u < NCH:
                 silu(u // 4, 2 * (u % 4) + 1)
-            if 0 <= tau - 1 < NCH:
-                fold(tau - 1)
-            if 0 <= tau - 2 < NCH:
-                sin_c(tau - 2)
-            if tau - 5 >= 0 and (tau - 5) % 4 == 0 and (tau - 5) // 4 < NT:
-                quant_f((tau - 5) // 4, 0)
-            if tau - 6 >= 0 and (tau - 6) % 4 == 0 and (tau - 6) // 4 < NT:
-                quant_f((tau - 6) // 4, 1)
-            for k in w_units:
-                w1_quant(k)
-            if tau == W_SLOT0 + 16 // W_PER_SLOT:
-                small_weights()
-            if u - 2 >= 0 and (u - 2) % 4 == 0 and (u - 2) // 4 < NT:
-                quant_h((u - 2) // 4, 0)
-            if u - 4 >= 0 and (u - 4) % 4 == 0 and (u - 4) // 4 < NT:
-                quant_h((u - 4) // 4, 1)
-            if u - 6 >= 0 and (u - 6) % 4 == 0 and (u - 6) // 4 < NT:
-                outx((u - 6) // 4)
+            if tau - 1 in slot_f:
+                fold(slot_f[tau - 1])
+            if tau - 2 in slot_f:
+                sin_c(slot_f[tau - 2])
+            for sp in range(2):
+                nt = tile_due(QF_LAG[sp])
+                if nt is not None:
+                    quant_f(nt, sp)
+            for g in range(2):
+                nt = tile_due(MLP_LAG + QH_LAG[g])
+                if nt is not None:
+                    quant_h(nt, g)
+            nt = tile_due(MLP_LAG + OUT_LAG)
+            if nt is not None:
+                outx(nt)

@@ -27,7 +27,7 @@ INV_2PI = 1.0 / (2.0 * math.pi)
 TWO_PI = 2.0 * math.pi
 OUT_SCALE = 1.0 / math.sqrt(128.0)
 
-ABS_ON_SCALAR = (1, 5)
+ABS_ON_SCALAR = (1, 3, 5, 7)
 Z_BUFS = 7
 O_BUFS = 1
 MLP_LAG = 9

@@ -27,15 +27,10 @@ INV_2PI = 1.0 / (2.0 * math.pi)
 TWO_PI = 2.0 * math.pi
 OUT_SCALE = 1.0 / math.sqrt(128.0)
 
-ABS_ON_SCALAR = (1, 3, 5, 7)
 Z_BUFS = 7
 O_BUFS = 1
-MLP_LAG = 9
-RG_LAG = (3, 5)
-QH_LAG = (4, 6)
-MM2_LAG = 7
-OUT_LAG = 8
-QF_LAG = (5, 6)
+W1_VECTOR = 5
+ABS_VECTOR = 1536
 PARK = PAIRS - P
 
 
@@ -48,14 +43,18 @@ def tile_gabtemplatemlp_t_kernel(tc, seq_len, freqs, W1, b1, W2, b2, dr, dc, out
         ps_z = ctx.enter_context(tc.psum_pool(name="ps_z", bufs=Z_BUFS))
         ps_o = ctx.enter_context(tc.psum_pool(name="ps_o", bufs=O_BUFS))
 
+        drf = dr.rearrange("i j -> (i j)")
+        dcf = dc.rearrange("i j -> (i j)")
+        frc = const.tile([P, 1], BF16)
+        nc.sync.dma_start(out=frc[:], in_=freqs.rearrange("(p o) -> p o", o=1))
+        dr0 = const.tile([P, 512], BF16)
+        nc.sync.dma_start(out=dr0[:], in_=drf[0:512].partition_broadcast(P))
+        dc0 = const.tile([P, 512], BF16)
+        nc.sync.dma_start(out=dc0[:], in_=dcf[0:512].partition_broadcast(P))
         drc = const.tile([P, 32], BF16)
-        nc.sync.dma_start(out=drc[:], in_=dr.rearrange("i j -> (i j)").rearrange("(q n) -> q n", n=32))
+        nc.sync.dma_start(out=drc[:], in_=drf.rearrange("(q n) -> q n", n=32))
         dcc = const.tile([P, 32], BF16)
-        nc.sync.dma_start(out=dcc[:], in_=dc.rearrange("i j -> (i j)").rearrange("(q n) -> q n", n=32))
-        brow = const.tile([P, P], BF16)
-        nc.vector.memset(brow[:], 0.0)
-        nc.sync.dma_start(out=brow[0:8, :], in_=b1.rearrange("(j p) -> j p", p=P))
-        nc.sync.dma_start(out=brow[8:9, :], in_=freqs.rearrange("(o p) -> o p", o=1))
+        nc.sync.dma_start(out=dcc[:], in_=dcf.rearrange("(q n) -> q n", n=32))
         w1raw = const.tile([P, 32, 256], BF16)
         w1v = W1.rearrange("h f -> (h f)").rearrange("(b q x) -> q b x", q=P, x=256)
 
@@ -63,33 +62,39 @@ def tile_gabtemplatemlp_t_kernel(tc, seq_len, freqs, W1, b1, W2, b2, dr, dc, out
             nc.sync.dma_start(out=w1raw[:, 8 * part:8 * part + 8, :], in_=w1v[:, 8 * part:8 * part + 8, :])
 
         load_w1(0)
+        load_w1(1)
+        brow = const.tile([P, P], BF16)
+        nc.gpsimd.memset(brow[:], 0.0)
+        nc.sync.dma_start(out=brow[0:8, :], in_=b1.rearrange("(j p) -> j p", p=P))
 
         x4 = const.tile([P, 32, 4], F32)
-        nc.vector.tensor_copy(out=x4[:, :, 0], in_=drc[:])
-        nc.vector.tensor_copy(out=x4[:, :, 1], in_=dcc[:])
-        nc.vector.tensor_tensor(out=x4[:, :, 2], in0=drc[:], in1=dcc[:], op=ALU.add)
-        nc.vector.tensor_tensor(out=x4[:, :, 3], in0=drc[:], in1=dcc[:], op=ALU.subtract)
         rows = out.rearrange("i j t -> (i j) t")
-        nc.sync.dma_start(out=rows[PARK:PAIRS, :], in_=x4[:].rearrange("q n t -> q (n t)"))
         parked = rows[PARK:PAIRS, :].rearrange("q x -> (q x)")
-        xs = const.tile([P, NT, 2048], F32)
+        xs = {}
 
-        def load_x(a, lo, hi):
-            nc.sync.dma_start(out=xs[:, a, lo:hi], in_=parked[2048 * a + lo:2048 * a + hi].partition_broadcast(P))
+        def park():
+            nc.gpsimd.tensor_copy(out=x4[:, :, 0], in_=drc[:])
+            nc.gpsimd.tensor_copy(out=x4[:, :, 1], in_=dcc[:])
+            nc.gpsimd.tensor_tensor(out=x4[:, :, 2], in0=drc[:], in1=dcc[:], op=ALU.add)
+            nc.gpsimd.tensor_tensor(out=x4[:, :, 3], in0=drc[:], in1=dcc[:], op=ALU.subtract)
+            nc.sync.dma_start(out=rows[PARK:PAIRS, :], in_=x4[:].rearrange("q n t -> q (n t)"))
 
-        load_w1(1)
-        load_w1(2)
-        load_x(0, 0, 512)
-        load_x(0, 512, 1024)
-        load_w1(3)
-        load_x(0, 1024, 2048)
+        def load_x(a):
+            xs[a] = work.tile([P, 2048], F32, tag="x", bufs=4, name="x")
+            nc.sync.dma_start(out=xs[a][:], in_=parked[2048 * a:2048 * a + 2048].partition_broadcast(P))
+
         w2raw = const.tile([P, HID], BF16)
-        nc.sync.dma_start(out=w2raw[:], in_=W2)
-        load_x(1, 0, 2048)
         b2b = const.tile([P, T], BF16)
-        nc.sync.dma_start(out=b2b[:], in_=b2.partition_broadcast(P))
-        for a in range(2, NT):
-            load_x(a, 0, 2048)
+
+        def later_loads():
+            load_x(1)
+            load_w1(2)
+            load_w1(3)
+            nc.sync.dma_start(out=w2raw[:], in_=W2)
+            load_x(2)
+            nc.sync.dma_start(out=b2b[:], in_=b2.partition_broadcast(P))
+            for a in range(3, NT):
+                load_x(a)
 
         warm = const.tile([P, 1], F32)
         nc.vector.memset(warm[:], 0.0)
@@ -120,50 +125,67 @@ def tile_gabtemplatemlp_t_kernel(tc, seq_len, freqs, W1, b1, W2, b2, dr, dc, out
         hgr = {}
         hq = {}
         oo = {}
+        osb = {}
         wts = {}
 
-        pieces_f = [(0, 512 * s, 512) for s in range(4)] + [(nt, 1024 * h, 1024) for nt in range(1, NT) for h in range(2)]
-        slot_f = {4 * nt + lo // 512: i for i, (nt, lo, n) in enumerate(pieces_f)}
+        sum0 = const.tile([P, 2, 512], F32)
+        r0 = work.tile([P, 2, 4, 256], F32, tag="r", bufs=2)
+        ab0 = work.tile([P, 2, 4, 256], F32, tag="ab", bufs=2)
 
-        def turns(i):
-            nt, lo, n = pieces_f[i]
-            kk[i] = work.tile([P, n], I32, tag="kk", bufs=3, name="kk")
-            nc.vector.tensor_scalar(out=kk[i][:], in0=xs[:, nt, lo:lo + n], scalar1=fcol[:, 0:1], scalar2=None, op0=ALU.mult)
+        def reduce_first(h):
+            lo, hi = 256 * h, 256 * h + 256
+            nc.vector.tensor_tensor(out=sum0[:, 0, lo:hi], in0=dr0[:, lo:hi], in1=dc0[:, lo:hi], op=ALU.add)
+            nc.vector.tensor_tensor(out=sum0[:, 1, lo:hi], in0=dr0[:, lo:hi], in1=dc0[:, lo:hi], op=ALU.subtract)
+            x = (dr0[:, lo:hi], dc0[:, lo:hi], sum0[:, 0, lo:hi], sum0[:, 1, lo:hi])
+            k0 = work.tile([P, 4, 256], I32, tag="k0", bufs=2)
+            for y in range(4):
+                nc.vector.tensor_scalar(out=k0[:, y, :], in0=x[y], scalar1=fcol[:, 0:1], scalar2=None, op0=ALU.mult)
+            for y in range(4):
+                nc.vector.scalar_tensor_tensor(out=r0[:, h, y, :], in0=x[y], scalar=fcol[:, 0:1], in1=k0[:, y, :],
+                                               op0=ALU.mult, op1=ALU.subtract)
 
-        def reduce(i):
-            nt, lo, n = pieces_f[i]
-            rr[i] = work.tile([P, n], F32, tag="r", bufs=3, name="r")
-            nc.vector.scalar_tensor_tensor(out=rr[i][:], in0=xs[:, nt, lo:lo + n], scalar=fcol[:, 0:1], in1=kk[i][:],
-                                           op0=ALU.mult, op1=ALU.subtract)
+        def sin_first(h):
+            if h == 0:
+                feat[0] = work.tile([P, 2, 2048], BF16, tag="f", bufs=2, align_bytes=64, name="f")
+            nc.scalar.activation(out=feat[0][:, 0, 1024 * h:1024 * h + 1024].rearrange("p (n y) -> p n y", y=4),
+                                 in_=r0[:, h, :, :].rearrange("p y n -> p n y"), func=ACT.Sin, scale=TWO_PI)
 
-        def sin_s(i):
-            nt, lo, n = pieces_f[i]
-            if lo == 0:
-                feat[(nt, 0)] = work.tile([P, 2048], BF16, tag="fs", bufs=2, align_bytes=64, name="fs")
-            nc.scalar.activation(out=feat[(nt, 0)][:, lo:lo + n], in_=rr[i][:], func=ACT.Sin, scale=TWO_PI)
+        def fold_first(h):
+            nc.scalar.activation(out=ab0[:, h, :, :], in_=r0[:, h, :, :], func=ACT.Abs)
 
-        def fold(i):
-            nt, lo, n = pieces_f[i]
-            ab[i] = work.tile([P, n], F32, tag="ab", bufs=3, name="ab")
-            if i % 8 in ABS_ON_SCALAR:
-                nc.scalar.activation(out=ab[i][:], in_=rr[i][:], func=ACT.Abs)
-            else:
-                nc.vector.scalar_tensor_tensor(out=ab[i][:], in0=rr[i][:], scalar=-1.0, in1=rr[i][:],
-                                               op0=ALU.mult, op1=ALU.max)
-
-        def sin_c(i):
-            nt, lo, n = pieces_f[i]
-            if lo == 0:
-                feat[(nt, 1)] = work.tile([P, 2048], BF16, tag="fc", bufs=2, align_bytes=64, name="fc")
-            nc.scalar.activation(out=feat[(nt, 1)][:, lo:lo + n], in_=ab[i][:], func=ACT.Sin,
+        def cos_first(h):
+            nc.scalar.activation(out=feat[0][:, 1, 1024 * h:1024 * h + 1024].rearrange("p (n y) -> p n y", y=4),
+                                 in_=ab0[:, h, :, :].rearrange("p y n -> p n y"), func=ACT.Sin,
                                  scale=-TWO_PI, bias=halfpi[:])
 
-        def quant_f(nt, sp):
-            if sp == 0:
-                fq[nt] = (work.tile([P, 2, 512], U32, tag="fqc", bufs=3, align_bytes=64, name="fqc"),
-                          work.tile([P, 2, 512], U8, tag="fqs", bufs=3, align_bytes=64, name="fqs"))
-            nc.vector.quantize_mx(out=fq[nt][0][:, sp, :].bitcast(FP8X4), scales=fq[nt][1][:, sp, :],
-                                  in_=feat[(nt, sp)][:])
+        def turns(nt):
+            kk[nt] = work.tile([P, 2048], I32, tag="kk", bufs=2, name="kk")
+            nc.vector.tensor_scalar(out=kk[nt][:], in0=xs[nt][:], scalar1=fcol[:, 0:1], scalar2=None, op0=ALU.mult)
+
+        def reduce(nt):
+            rr[nt] = work.tile([P, 2048], F32, tag="r", bufs=2, name="r")
+            nc.vector.scalar_tensor_tensor(out=rr[nt][:], in0=xs[nt][:], scalar=fcol[:, 0:1], in1=kk[nt][:],
+                                           op0=ALU.mult, op1=ALU.subtract)
+
+        def sin_s(nt):
+            feat[nt] = work.tile([P, 2, 2048], BF16, tag="f", bufs=2, align_bytes=64, name="f")
+            nc.scalar.activation(out=feat[nt][:, 0, :], in_=rr[nt][:], func=ACT.Sin, scale=TWO_PI)
+
+        def fold(nt):
+            ab[nt] = work.tile([P, 2048], F32, tag="ab", bufs=2, name="ab")
+            nc.vector.scalar_tensor_tensor(out=ab[nt][:, 0:ABS_VECTOR], in0=rr[nt][:, 0:ABS_VECTOR], scalar=-1.0,
+                                           in1=rr[nt][:, 0:ABS_VECTOR], op0=ALU.mult, op1=ALU.max)
+            nc.scalar.activation(out=ab[nt][:, ABS_VECTOR:2048], in_=rr[nt][:, ABS_VECTOR:2048], func=ACT.Abs)
+
+        def sin_c(nt):
+            nc.scalar.activation(out=feat[nt][:, 1, :], in_=ab[nt][:], func=ACT.Sin, scale=-TWO_PI, bias=halfpi[:])
+
+        def quant_f(nt):
+            fq[nt] = (work.tile([P, 2, 512], U32, tag="fqc", bufs=2, align_bytes=64, name="fqc"),
+                      work.tile([P, 2, 512], U8, tag="fqs", bufs=2, align_bytes=64, name="fqs"))
+            nc.vector.quantize_mx(out=fq[nt][0][:].rearrange("p h n -> p (h n)").bitcast(FP8X4),
+                                  scales=fq[nt][1][:].rearrange("p h n -> p (h n)"),
+                                  in_=feat[nt][:].rearrange("p h n -> p (h n)"))
 
         def w1_pe(u):
             j, sp = u // 2, u % 2
@@ -173,8 +195,8 @@ def tile_gabtemplatemlp_t_kernel(tc, seq_len, freqs, W1, b1, W2, b2, dr, dc, out
                                     in_=w1raw[:, 4 * j + b, P * sp:P * sp + P], identity=ident[:])
 
         def w1_exit(u):
-            wg = work.tile([P, 512], BF16, tag="wg", bufs=4, align_bytes=64)
-            if u % 2 == 0:
+            wg = work.tile([P, 512], BF16, tag="wg", bufs=12, align_bytes=64)
+            if u >= W1_VECTOR:
                 nc.scalar.copy(out=wg[:], in_=wts[u][:])
             else:
                 nc.vector.tensor_copy(out=wg[:], in_=wts[u][:])
@@ -188,7 +210,6 @@ def tile_gabtemplatemlp_t_kernel(tc, seq_len, freqs, W1, b1, W2, b2, dr, dc, out
         def columns():
             bt = ps_z.tile([P, P], BF16, tag="z")
             nc.tensor.transpose(out=bt[:], in_=brow[:], identity=ident[:])
-            nc.vector.tensor_scalar(out=fcol[:], in0=bt[:, MT:MT + 1], scalar1=INV_2PI, scalar2=None, op0=ALU.mult)
             nc.vector.tensor_copy(out=b1c[:], in_=bt[:, 0:MT])
 
         def small_weights():
@@ -217,35 +238,38 @@ def tile_gabtemplatemlp_t_kernel(tc, seq_len, freqs, W1, b1, W2, b2, dr, dc, out
                     start=(sp == 0), stop=(sp == 1),
                 )
 
-        def silu(nt, j):
-            if j == 0:
+        def silu(nt, j, lo=0, hi=512):
+            if nt not in hpl:
                 hpl[nt] = work.tile([P, MT, 512], BF16, tag="hpl", bufs=2, name="hpl")
-            nc.scalar.activation(out=hpl[nt][:, j, :], in_=zz[(nt, j)][:], func=ACT.Silu, bias=b1c[:, j:j + 1])
+            nc.scalar.activation(out=hpl[nt][:, j, lo:hi], in_=zz[(nt, j)][:, lo:hi], func=ACT.Silu, bias=b1c[:, j:j + 1])
 
-        def pieces(nt, g):
-            if nt == NT - 1 and g == 1:
-                return [(0, 256), (256, 512)]
-            return [(0, 512)]
-
-        def regroup(nt, g):
-            hgr[(nt, g)] = work.tile([P, 512, 4], BF16, tag="hg", bufs=3, align_bytes=64, name="hg")
-            for lo, hi in pieces(nt, g):
-                nc.vector.tensor_copy(
-                    out=hgr[(nt, g)][:, lo:hi, :].rearrange("p (c i) t -> p c t i", i=4),
-                    in_=hpl[nt][:, 4 * g:4 * g + 4, lo:hi].rearrange("p t (c i) -> p c t i", i=4),
-                )
-
-        def quant_h(nt, g):
-            if g == 0:
+        def hq_tiles(nt):
+            if nt not in hq:
+                hgr[nt] = work.tile([P, 2, 512, 4], BF16, tag="hg", bufs=3, align_bytes=64, name="hg")
                 hq[nt] = (work.tile([P, 2, 512], U32, tag="hc", bufs=2, align_bytes=64, name="hc"),
                           work.tile([P, 2, 512], U8, tag="hs", bufs=2, align_bytes=64, name="hs"))
-            for lo, hi in pieces(nt, g):
-                nc.vector.quantize_mx(out=hq[nt][0][:, g, lo:hi].bitcast(FP8X4), scales=hq[nt][1][:, g, lo:hi],
-                                      in_=hgr[(nt, g)][:, lo:hi, :].rearrange("p w t -> p (w t)"))
+
+        def quant_h(nt):
+            nc.vector.quantize_mx(out=hq[nt][0][:].rearrange("p g n -> p (g n)").bitcast(FP8X4),
+                                  scales=hq[nt][1][:].rearrange("p g n -> p (g n)"),
+                                  in_=hgr[nt][:].rearrange("p g n t -> p (g n t)"))
+
+        def regroup(nt, g, lo, hi):
+            hq_tiles(nt)
+            nc.vector.tensor_copy(
+                out=hgr[nt][:, g, lo:hi, :].rearrange("p (c i) t -> p c t i", i=4),
+                in_=hpl[nt][:, 4 * g:4 * g + 4, lo:hi].rearrange("p t (c i) -> p c t i", i=4))
+
+        def quant_part(nt, g, lo, hi):
+            nc.vector.quantize_mx(out=hq[nt][0][:, g, lo:hi].bitcast(FP8X4), scales=hq[nt][1][:, g, lo:hi],
+                                  in_=hgr[nt][:, g, lo:hi, :].rearrange("p n t -> p (n t)"))
 
         def mm2(nt):
             oo[nt] = ps_o.tile([P, SUB, T], F32, tag="o", name="o")
-            for s in range(SUB):
+            mm2_part(nt, 0, SUB)
+
+        def mm2_part(nt, a, b):
+            for s in range(a, b):
                 for g in range(2):
                     nc.tensor.matmul_mx(
                         out=oo[nt][:, s, :],
@@ -256,14 +280,13 @@ def tile_gabtemplatemlp_t_kernel(tc, seq_len, freqs, W1, b1, W2, b2, dr, dc, out
                         start=(g == 0), stop=(g == 1),
                     )
 
-        def outx(nt):
-            osb = work.tile([P, SUB, T], F32, tag="osb", bufs=3)
-            for lo, hi in pieces(nt, 1):
-                a, b = lo // P, hi // P
-                nc.vector.scalar_tensor_tensor(out=osb[:, a:b, :], in0=oo[nt][:, a:b, :], scalar=OUT_SCALE,
-                                               in1=b2s[:].unsqueeze(1).to_broadcast([P, b - a, T]),
-                                               op0=ALU.mult, op1=ALU.add)
-                nc.sync.dma_start(out=outv[nt][:, a:b, :], in_=osb[:, a:b, :])
+        def outx(nt, a=0, b=SUB):
+            if a == 0:
+                osb[nt] = work.tile([P, SUB, T], F32, tag="osb", bufs=2, name="osb")
+            nc.vector.scalar_tensor_tensor(out=osb[nt][:, a:b, :], in0=oo[nt][:, a:b, :], scalar=OUT_SCALE,
+                                           in1=b2s[:].unsqueeze(1).to_broadcast([P, b - a, T]),
+                                           op0=ALU.mult, op1=ALU.add)
+            nc.sync.dma_start(out=outv[nt][:, a:b, :], in_=osb[nt][:, a:b, :])
 
         def w1_units(lo, hi):
             for k in range(lo, hi):
@@ -272,54 +295,80 @@ def tile_gabtemplatemlp_t_kernel(tc, seq_len, freqs, W1, b1, W2, b2, dr, dc, out
                 if k >= 2:
                     w1_quant(k - 2)
 
+        def has(nt):
+            return 0 <= nt < NT
+
+        nc.vector.tensor_scalar(out=fcol[:], in0=frc[:], scalar1=INV_2PI, scalar2=None, op0=ALU.mult)
+        park()
+        later_loads()
+        reduce_first(0)
+        sin_first(0)
+        fold_first(0)
+        reduce_first(1)
+        cos_first(0)
+        sin_first(1)
+        fold_first(1)
+        w1_units(0, W1_VECTOR)
+        cos_first(1)
+        turns(1)
+        w1_units(W1_VECTOR, 8)
+        reduce(1)
+        w1_units(8, 16)
         columns()
-        w1_units(0, 12)
-        turns(0)
-        for tau in range(NCH + MLP_LAG + OUT_LAG + 1):
-            u = tau - MLP_LAG
+        sin_s(1)
+        quant_f(0)
+        for j in range(4):
+            mm1(0, j)
+        w1_quant(14)
+        w1_quant(15)
+        fold(1)
+        for j in range(4, 7):
+            mm1(0, j)
+        turns(2)
 
-            def tile_due(lag, t=tau):
-                return (t - lag) // 4 if (t - lag) >= 0 and (t - lag) % 4 == 0 and (t - lag) // 4 < NT else None
-
-            if 1 <= tau <= 2:
-                w1_units(10 + 2 * tau, 12 + 2 * tau)
-            if tau == 3:
-                w1_quant(14)
-                w1_quant(15)
-            if tau == 5:
+        for per in range(1, NT + 1):
+            mm1(per - 1, 7)
+            if has(per - 2):
+                regroup(per - 2, 1, 0, 512)
+            if has(per + 1):
+                reduce(per + 1)
+            if per == 1:
                 small_weights()
-            if 0 <= u < NCH:
-                mm1(u // 4, 2 * (u % 4))
-                mm1(u // 4, 2 * (u % 4) + 1)
-            nt = tile_due(MLP_LAG + MM2_LAG)
-            if nt is not None:
-                mm2(nt)
-            if tau in slot_f:
-                reduce(slot_f[tau])
-            for g in range(2):
-                nt = tile_due(MLP_LAG + RG_LAG[g])
-                if nt is not None:
-                    regroup(nt, g)
-            if tau in slot_f and slot_f[tau] + 1 < len(pieces_f):
-                turns(slot_f[tau] + 1)
-            if 0 <= u < NCH:
-                silu(u // 4, 2 * (u % 4))
-            if tau - 1 in slot_f:
-                sin_s(slot_f[tau - 1])
-            if 0 <= u < NCH:
-                silu(u // 4, 2 * (u % 4) + 1)
-            if tau - 1 in slot_f:
-                fold(slot_f[tau - 1])
-            if tau - 2 in slot_f:
-                sin_c(slot_f[tau - 2])
-            for sp in range(2):
-                nt = tile_due(QF_LAG[sp])
-                if nt is not None:
-                    quant_f(nt, sp)
-            for g in range(2):
-                nt = tile_due(MLP_LAG + QH_LAG[g])
-                if nt is not None:
-                    quant_h(nt, g)
-            nt = tile_due(MLP_LAG + OUT_LAG)
-            if nt is not None:
-                outx(nt)
+            if has(per - 2):
+                quant_h(per - 2)
+                mm2(per - 2)
+            silu(per - 1, 0)
+            silu(per - 1, 1)
+            if has(per):
+                sin_c(per)
+            silu(per - 1, 2)
+            silu(per - 1, 3)
+            if has(per):
+                quant_f(per)
+                for j in range(4):
+                    mm1(per, j)
+            if has(per + 1):
+                sin_s(per + 1)
+                fold(per + 1)
+            regroup(per - 1, 0, 0, 512)
+            if has(per + 2):
+                turns(per + 2)
+            if has(per - 2):
+                outx(per - 2)
+            if per < NT:
+                for j in range(4, 8):
+                    silu(per - 1, j)
+            if has(per):
+                for j in range(4, 7):
+                    mm1(per, j)
+        for lo, hi in ((0, 256), (256, 512)):
+            for j in range(4, 8):
+                silu(NT - 1, j, lo, hi)
+        quant_part(NT - 1, 0, 0, 512)
+        oo[NT - 1] = ps_o.tile([P, SUB, T], F32, tag="o", name="o")
+        for lo, hi in ((0, 256), (256, 512)):
+            regroup(NT - 1, 1, lo, hi)
+            quant_part(NT - 1, 1, lo, hi)
+            mm2_part(NT - 1, lo // P, hi // P)
+        for lo, hi in ((0, 256), (256, 512)):
+            outx(NT - 1, lo // P, hi // P)

@@ -29,7 +29,7 @@ OUT_SCALE = 1.0 / math.sqrt(128.0)
 
 Z_BUFS = 7
 O_BUFS = 1
-W1_VECTOR = 5
+W1_VECTOR = 8
 ABS_VECTOR = 1536
 PARK = PAIRS - P
 
@@ -45,27 +45,28 @@ def tile_gabtemplatemlp_t_kernel(tc, seq_len, freqs, W1, b1, W2, b2, dr, dc, out
 
         drf = dr.rearrange("i j -> (i j)")
         dcf = dc.rearrange("i j -> (i j)")
+        drc = const.tile([P, 32], BF16)
+        nc.sync.dma_start(out=drc[:], in_=drf.rearrange("(q n) -> q n", n=32))
+        dcc = const.tile([P, 32], BF16)
+        nc.sync.dma_start(out=dcc[:], in_=dcf.rearrange("(q n) -> q n", n=32))
         frc = const.tile([P, 1], BF16)
         nc.sync.dma_start(out=frc[:], in_=freqs.rearrange("(p o) -> p o", o=1))
         dr0 = const.tile([P, 512], BF16)
         nc.sync.dma_start(out=dr0[:], in_=drf[0:512].partition_broadcast(P))
         dc0 = const.tile([P, 512], BF16)
         nc.sync.dma_start(out=dc0[:], in_=dcf[0:512].partition_broadcast(P))
-        drc = const.tile([P, 32], BF16)
-        nc.sync.dma_start(out=drc[:], in_=drf.rearrange("(q n) -> q n", n=32))
-        dcc = const.tile([P, 32], BF16)
-        nc.sync.dma_start(out=dcc[:], in_=dcf.rearrange("(q n) -> q n", n=32))
         w1raw = const.tile([P, 32, 256], BF16)
         w1v = W1.rearrange("h f -> (h f)").rearrange("(b q x) -> q b x", q=P, x=256)
+        brow = const.tile([P, P], BF16)
+        nc.gpsimd.memset(brow[:], 0.0)
 
         def load_w1(part):
             nc.sync.dma_start(out=w1raw[:, 8 * part:8 * part + 8, :], in_=w1v[:, 8 * part:8 * part + 8, :])
 
         load_w1(0)
-        load_w1(1)
-        brow = const.tile([P, P], BF16)
-        nc.gpsimd.memset(brow[:], 0.0)
-        nc.sync.dma_start(out=brow[0:8, :], in_=b1.rearrange("(j p) -> j p", p=P))
+        warm = const.tile([P, 1], F32)
+        nc.vector.memset(warm[:], 0.0)
+        nc.scalar.activation(out=warm[:], in_=warm[:], func=ACT.Silu)
 
         x4 = const.tile([P, 32, 4], F32)
         rows = out.rearrange("i j t -> (i j) t")
@@ -73,10 +74,10 @@ def tile_gabtemplatemlp_t_kernel(tc, seq_len, freqs, W1, b1, W2, b2, dr, dc, out
         xs = {}
 
         def park():
-            nc.gpsimd.tensor_copy(out=x4[:, :, 0], in_=drc[:])
-            nc.gpsimd.tensor_copy(out=x4[:, :, 1], in_=dcc[:])
-            nc.gpsimd.tensor_tensor(out=x4[:, :, 2], in0=drc[:], in1=dcc[:], op=ALU.add)
-            nc.gpsimd.tensor_tensor(out=x4[:, :, 3], in0=drc[:], in1=dcc[:], op=ALU.subtract)
+            nc.vector.tensor_copy(out=x4[:, :, 0], in_=drc[:])
+            nc.vector.tensor_copy(out=x4[:, :, 1], in_=dcc[:])
+            nc.vector.tensor_tensor(out=x4[:, :, 2], in0=drc[:], in1=dcc[:], op=ALU.add)
+            nc.vector.tensor_tensor(out=x4[:, :, 3], in0=drc[:], in1=dcc[:], op=ALU.subtract)
             nc.sync.dma_start(out=rows[PARK:PAIRS, :], in_=x4[:].rearrange("q n t -> q (n t)"))
 
         def load_x(a):
@@ -87,18 +88,17 @@ def tile_gabtemplatemlp_t_kernel(tc, seq_len, freqs, W1, b1, W2, b2, dr, dc, out
         b2b = const.tile([P, T], BF16)
 
         def later_loads():
-            load_x(1)
+            load_w1(1)
             load_w1(2)
+            load_x(1)
             load_w1(3)
+            nc.sync.dma_start(out=brow[0:8, :], in_=b1.rearrange("(j p) -> j p", p=P))
             nc.sync.dma_start(out=w2raw[:], in_=W2)
             load_x(2)
             nc.sync.dma_start(out=b2b[:], in_=b2.partition_broadcast(P))
             for a in range(3, NT):
                 load_x(a)
 
-        warm = const.tile([P, 1], F32)
-        nc.vector.memset(warm[:], 0.0)
-        nc.scalar.activation(out=warm[:], in_=warm[:], func=ACT.Silu)
         ident = const.tile([P, P], BF16)
         make_identity(nc, ident[:])
         one = const.tile([P, 1], F32)
@@ -122,6 +122,7 @@ def tile_gabtemplatemlp_t_kernel(tc, seq_len, freqs, W1, b1, W2, b2, dr, dc, out
         feat = {}
         zz = {}
         hpl = {}
+        hlast = {}
         hgr = {}
         hq = {}
         oo = {}
@@ -238,10 +239,21 @@ def tile_gabtemplatemlp_t_kernel(tc, seq_len, freqs, W1, b1, W2, b2, dr, dc, out
                     start=(sp == 0), stop=(sp == 1),
                 )
 
-        def silu(nt, j, lo=0, hi=512):
+        def silu(nt, j):
             if nt not in hpl:
                 hpl[nt] = work.tile([P, MT, 512], BF16, tag="hpl", bufs=2, name="hpl")
-            nc.scalar.activation(out=hpl[nt][:, j, lo:hi], in_=zz[(nt, j)][:, lo:hi], func=ACT.Silu, bias=b1c[:, j:j + 1])
+            nc.scalar.activation(out=hpl[nt][:, j, :], in_=zz[(nt, j)][:], func=ACT.Silu, bias=b1c[:, j:j + 1])
+
+        def silu_last(h, j):
+            if h not in hlast:
+                hlast[h] = work.tile([P, 4, 256], BF16, tag="hlast", bufs=2, name="hlast")
+            nc.scalar.activation(out=hlast[h][:, j - 4, :], in_=zz[(NT - 1, j)][:, 256 * h:256 * h + 256], func=ACT.Silu,
+                                 bias=b1c[:, j:j + 1])
+
+        def regroup_last(h):
+            nc.vector.tensor_copy(
+                out=hgr[NT - 1][:, 1, 256 * h:256 * h + 256, :].rearrange("p (c i) t -> p c t i", i=4),
+                in_=hlast[h][:].rearrange("p t (c i) -> p c t i", i=4))
 
         def hq_tiles(nt):
             if nt not in hq:
@@ -254,11 +266,11 @@ def tile_gabtemplatemlp_t_kernel(tc, seq_len, freqs, W1, b1, W2, b2, dr, dc, out
                                   scales=hq[nt][1][:].rearrange("p g n -> p (g n)"),
                                   in_=hgr[nt][:].rearrange("p g n t -> p (g n t)"))
 
-        def regroup(nt, g, lo, hi):
+        def regroup(nt, g):
             hq_tiles(nt)
             nc.vector.tensor_copy(
-                out=hgr[nt][:, g, lo:hi, :].rearrange("p (c i) t -> p c t i", i=4),
-                in_=hpl[nt][:, 4 * g:4 * g + 4, lo:hi].rearrange("p t (c i) -> p c t i", i=4))
+                out=hgr[nt][:, g, :, :].rearrange("p (c i) t -> p c t i", i=4),
+                in_=hpl[nt][:, 4 * g:4 * g + 4, :].rearrange("p t (c i) -> p c t i", i=4))
 
         def quant_part(nt, g, lo, hi):
             nc.vector.quantize_mx(out=hq[nt][0][:, g, lo:hi].bitcast(FP8X4), scales=hq[nt][1][:, g, lo:hi],
@@ -298,9 +310,9 @@ def tile_gabtemplatemlp_t_kernel(tc, seq_len, freqs, W1, b1, W2, b2, dr, dc, out
         def has(nt):
             return 0 <= nt < NT
 
-        nc.vector.tensor_scalar(out=fcol[:], in0=frc[:], scalar1=INV_2PI, scalar2=None, op0=ALU.mult)
         park()
         later_loads()
+        nc.vector.tensor_scalar(out=fcol[:], in0=frc[:], scalar1=INV_2PI, scalar2=None, op0=ALU.mult)
         reduce_first(0)
         sin_first(0)
         fold_first(0)
@@ -311,16 +323,19 @@ def tile_gabtemplatemlp_t_kernel(tc, seq_len, freqs, W1, b1, W2, b2, dr, dc, out
         w1_units(0, W1_VECTOR)
         cos_first(1)
         turns(1)
-        w1_units(W1_VECTOR, 8)
+        w1_quant(W1_VECTOR - 2)
+        w1_quant(W1_VECTOR - 1)
         reduce(1)
-        w1_units(8, 16)
+        for k in range(W1_VECTOR, 16):
+            w1_pe(k)
+            w1_exit(k)
         columns()
         sin_s(1)
         quant_f(0)
+        for k in range(W1_VECTOR, 16):
+            w1_quant(k)
         for j in range(4):
             mm1(0, j)
-        w1_quant(14)
-        w1_quant(15)
         fold(1)
         for j in range(4, 7):
             mm1(0, j)
@@ -329,13 +344,16 @@ def tile_gabtemplatemlp_t_kernel(tc, seq_len, freqs, W1, b1, W2, b2, dr, dc, out
         for per in range(1, NT + 1):
             mm1(per - 1, 7)
             if has(per - 2):
-                regroup(per - 2, 1, 0, 512)
+                regroup(per - 2, 1)
             if has(per + 1):
                 reduce(per + 1)
             if per == 1:
                 small_weights()
             if has(per - 2):
-                quant_h(per - 2)
+                if per < NT:
+                    quant_h(per - 2)
+                else:
+                    quant_part(per - 2, 1, 0, 512)
                 mm2(per - 2)
             silu(per - 1, 0)
             silu(per - 1, 1)
@@ -350,9 +368,11 @@ def tile_gabtemplatemlp_t_kernel(tc, seq_len, freqs, W1, b1, W2, b2, dr, dc, out
             if has(per + 1):
                 sin_s(per + 1)
                 fold(per + 1)
-            regroup(per - 1, 0, 0, 512)
+            regroup(per - 1, 0)
             if has(per + 2):
                 turns(per + 2)
+            if per == NT - 1:
+                quant_part(per - 1, 0, 0, 512)
             if has(per - 2):
                 outx(per - 2)
             if per < NT:
@@ -361,14 +381,14 @@ def tile_gabtemplatemlp_t_kernel(tc, seq_len, freqs, W1, b1, W2, b2, dr, dc, out
             if has(per):
                 for j in range(4, 7):
                     mm1(per, j)
-        for lo, hi in ((0, 256), (256, 512)):
+        for h in range(2):
             for j in range(4, 8):
-                silu(NT - 1, j, lo, hi)
+                silu_last(h, j)
         quant_part(NT - 1, 0, 0, 512)
         oo[NT - 1] = ps_o.tile([P, SUB, T], F32, tag="o", name="o")
-        for lo, hi in ((0, 256), (256, 512)):
-            regroup(NT - 1, 1, lo, hi)
-            quant_part(NT - 1, 1, lo, hi)
-            mm2_part(NT - 1, lo // P, hi // P)
-        for lo, hi in ((0, 256), (256, 512)):
-            outx(NT - 1, lo // P, hi // P)
+        for h in range(2):
+            regroup_last(h)
+            quant_part(NT - 1, 1, 256 * h, 256 * h + 256)
+            mm2_part(NT - 1, 2 * h, 2 * h + 2)
+        for h in range(2):
+            outx(NT - 1, 2 * h, 2 * h + 2)

@@ -30,6 +30,7 @@ OUT_SCALE = 1.0 / math.sqrt(128.0)
 Z_BUFS = 7
 O_BUFS = 1
 W1_VECTOR = 8
+GP_COLS = 256
 ABS_VECTOR = 1536
 PARK = PAIRS - P
 
@@ -123,6 +124,7 @@ def tile_gabtemplatemlp_t_kernel(tc, seq_len, freqs, W1, b1, W2, b2, dr, dc, out
         zz = {}
         hpl = {}
         hlast = {}
+        hgq = {}
         hgr = {}
         hq = {}
         oo = {}
@@ -174,8 +176,8 @@ def tile_gabtemplatemlp_t_kernel(tc, seq_len, freqs, W1, b1, W2, b2, dr, dc, out
 
         def fold(nt):
             ab[nt] = work.tile([P, 2048], F32, tag="ab", bufs=2, name="ab")
-            nc.vector.scalar_tensor_tensor(out=ab[nt][:, 0:ABS_VECTOR], in0=rr[nt][:, 0:ABS_VECTOR], scalar=-1.0,
-                                           in1=rr[nt][:, 0:ABS_VECTOR], op0=ALU.mult, op1=ALU.max)
+            nc.vector.tensor_reduce(out=ab[nt][:, 0:ABS_VECTOR], in_=rr[nt][:, 0:ABS_VECTOR].unsqueeze(2),
+                                    axis=mybir.AxisListType.X, op=ALU.max, apply_absolute_value=True)
             nc.scalar.activation(out=ab[nt][:, ABS_VECTOR:2048], in_=rr[nt][:, ABS_VECTOR:2048], func=ACT.Abs)
 
         def sin_c(nt):
@@ -261,16 +263,27 @@ def tile_gabtemplatemlp_t_kernel(tc, seq_len, freqs, W1, b1, W2, b2, dr, dc, out
                 hq[nt] = (work.tile([P, 2, 512], U32, tag="hc", bufs=2, align_bytes=64, name="hc"),
                           work.tile([P, 2, 512], U8, tag="hs", bufs=2, align_bytes=64, name="hs"))
 
-        def quant_h(nt):
-            nc.vector.quantize_mx(out=hq[nt][0][:].rearrange("p g n -> p (g n)").bitcast(FP8X4),
-                                  scales=hq[nt][1][:].rearrange("p g n -> p (g n)"),
-                                  in_=hgr[nt][:].rearrange("p g n t -> p (g n t)"))
-
         def regroup(nt, g):
             hq_tiles(nt)
             nc.vector.tensor_copy(
                 out=hgr[nt][:, g, :, :].rearrange("p (c i) t -> p c t i", i=4),
                 in_=hpl[nt][:, 4 * g:4 * g + 4, :].rearrange("p t (c i) -> p c t i", i=4))
+
+        def regroup_shared(nt):
+            hq_tiles(nt)
+            hgq[nt] = work.tile([P, GP_COLS, 4], BF16, tag="hgq", bufs=1, align_bytes=64, name="hgq")
+            nc.gpsimd.tensor_scalar(out=hgq[nt][:].rearrange("p (c i) t -> p c t i", i=4),
+                                    in0=hpl[nt][:, 0:4, 0:GP_COLS].rearrange("p t (c i) -> p c t i", i=4),
+                                    scalar1=1.0, scalar2=0.0, op0=ALU.mult, op1=ALU.add)
+            nc.vector.tensor_copy(
+                out=hgr[nt][:, 0, GP_COLS:512, :].rearrange("p (c i) t -> p c t i", i=4),
+                in_=hpl[nt][:, 0:4, GP_COLS:512].rearrange("p t (c i) -> p c t i", i=4))
+
+        def quant_shared(nt):
+            quant_part(nt, 1, 0, 512)
+            quant_part(nt, 0, GP_COLS, 512)
+            nc.vector.quantize_mx(out=hq[nt][0][:, 0, 0:GP_COLS].bitcast(FP8X4), scales=hq[nt][1][:, 0, 0:GP_COLS],
+                                  in_=hgq[nt][:].rearrange("p n t -> p (n t)"))
 
         def quant_part(nt, g, lo, hi):
             nc.vector.quantize_mx(out=hq[nt][0][:, g, lo:hi].bitcast(FP8X4), scales=hq[nt][1][:, g, lo:hi],
@@ -349,11 +362,11 @@ def tile_gabtemplatemlp_t_kernel(tc, seq_len, freqs, W1, b1, W2, b2, dr, dc, out
                 reduce(per + 1)
             if per == 1:
                 small_weights()
-            if has(per - 2):
-                if per < NT:
-                    quant_h(per - 2)
-                else:
-                    quant_part(per - 2, 1, 0, 512)
+            if per == NT - 1:
+                quant_shared(per - 2)
+                mm2(per - 2)
+            if per == NT:
+                quant_part(per - 2, 1, 0, 512)
                 mm2(per - 2)
             silu(per - 1, 0)
             silu(per - 1, 1)
@@ -363,18 +376,27 @@ def tile_gabtemplatemlp_t_kernel(tc, seq_len, freqs, W1, b1, W2, b2, dr, dc, out
             silu(per - 1, 3)
             if has(per):
                 quant_f(per)
+            if has(per - 2) and per < NT - 1:
+                quant_shared(per - 2)
+                mm2(per - 2)
+            if has(per):
                 for j in range(4):
                     mm1(per, j)
             if has(per + 1):
                 sin_s(per + 1)
                 fold(per + 1)
-            regroup(per - 1, 0)
+            if has(per - 2) and per < NT:
+                outx(per - 2)
+            if per < NT - 1:
+                regroup_shared(per - 1)
+            else:
+                regroup(per - 1, 0)
+            if per == NT:
+                outx(per - 2)
             if has(per + 2):
                 turns(per + 2)
             if per == NT - 1:
                 quant_part(per - 1, 0, 0, 512)
-            if has(per - 2):
-                outx(per - 2)
             if per < NT:
                 for j in range(4, 8):
                     silu(per - 1, j)
@@ -384,10 +406,11 @@ def tile_gabtemplatemlp_t_kernel(tc, seq_len, freqs, W1, b1, W2, b2, dr, dc, out
         for h in range(2):
             for j in range(4, 8):
                 silu_last(h, j)
+        regroup_last(0)
         quant_part(NT - 1, 0, 0, 512)
+        regroup_last(1)
         oo[NT - 1] = ps_o.tile([P, SUB, T], F32, tag="o", name="o")
         for h in range(2):
-            regroup_last(h)
             quant_part(NT - 1, 1, 256 * h, 256 * h + 256)
             mm2_part(NT - 1, 2 * h, 2 * h + 2)
         for h in range(2):

@@ -29,7 +29,7 @@ OUT_SCALE = 1.0 / math.sqrt(128.0)
 
 Z_BUFS = 7
 O_BUFS = 1
-W1_VECTOR = 8
+W1_VECTOR = 6
 GP_COLS = 256
 ABS_VECTOR = 1536
 PARK = PAIRS - P
@@ -128,7 +128,8 @@ def tile_gabtemplatemlp_t_kernel(tc, seq_len, freqs, W1, b1, W2, b2, dr, dc, out
         hgr = {}
         hq = {}
         oo = {}
-        osb = {}
+        olast = {}
+        w2t = {}
         wts = {}
 
         sum0 = const.tile([P, 2, 512], F32)
@@ -215,16 +216,19 @@ def tile_gabtemplatemlp_t_kernel(tc, seq_len, freqs, W1, b1, W2, b2, dr, dc, out
             nc.tensor.transpose(out=bt[:], in_=brow[:], identity=ident[:])
             nc.vector.tensor_copy(out=b1c[:], in_=bt[:, 0:MT])
 
+        def w2_pe():
+            for g in range(2):
+                w2t[g] = ps_z.tile([P, 4, P], BF16, tag="z", name="w2t")
+                for t in range(4):
+                    nc.tensor.transpose(out=w2t[g][:, t, :], in_=w2raw[:, P * (4 * g + t):P * (4 * g + t) + P],
+                                        identity=ident[:])
+
         def small_weights():
             nc.vector.tensor_scalar(out=b2s[:], in0=b2b[:], scalar1=OUT_SCALE, scalar2=None, op0=ALU.mult)
             w2g = {}
             for g in range(2):
-                w2t = ps_z.tile([P, 4, P], BF16, tag="z")
-                for t in range(4):
-                    nc.tensor.transpose(out=w2t[:, t, :], in_=w2raw[:, P * (4 * g + t):P * (4 * g + t) + P],
-                                        identity=ident[:])
                 w2g[g] = work.tile([P, P, 4], BF16, tag="w2g", bufs=2, align_bytes=64, name="w2g")
-                nc.vector.tensor_copy(out=w2g[g][:], in_=w2t[:].rearrange("p t c -> p c t"))
+                nc.vector.tensor_copy(out=w2g[g][:], in_=w2t[g][:].rearrange("p t c -> p c t"))
             for g in range(2):
                 nc.vector.quantize_mx(out=w2c[:, g, :].bitcast(FP8X4), scales=w2s[:, g, :],
                                       in_=w2g[g][:].rearrange("p c t -> p (c t)"))
@@ -291,13 +295,17 @@ def tile_gabtemplatemlp_t_kernel(tc, seq_len, freqs, W1, b1, W2, b2, dr, dc, out
 
         def mm2(nt):
             oo[nt] = ps_o.tile([P, SUB, T], F32, tag="o", name="o")
-            mm2_part(nt, 0, SUB)
+            mm2_into(oo[nt], nt, 0, SUB)
 
-        def mm2_part(nt, a, b):
+        def mm2_last(h):
+            olast[h] = ps_z.tile([P, 2, T], F32, tag="z", name="olast")
+            mm2_into(olast[h], NT - 1, 2 * h, 2 * h + 2)
+
+        def mm2_into(o, nt, a, b):
             for s in range(a, b):
                 for g in range(2):
                     nc.tensor.matmul_mx(
-                        out=oo[nt][:, s, :],
+                        out=o[:, s - a, :],
                         lhsT=hq[nt][0][:, g, P * s:P * s + P].bitcast(FP8X4),
                         lhsT_scale=hq[nt][1][:, g, P * s:P * s + P],
                         rhs=w2c[:, g, :].bitcast(FP8X4),
@@ -305,13 +313,18 @@ def tile_gabtemplatemlp_t_kernel(tc, seq_len, freqs, W1, b1, W2, b2, dr, dc, out
                         start=(g == 0), stop=(g == 1),
                     )
 
-        def outx(nt, a=0, b=SUB):
-            if a == 0:
-                osb[nt] = work.tile([P, SUB, T], F32, tag="osb", bufs=2, name="osb")
-            nc.vector.scalar_tensor_tensor(out=osb[nt][:, a:b, :], in0=oo[nt][:, a:b, :], scalar=OUT_SCALE,
+        def out_from(o, nt, a, b):
+            osb = work.tile([P, b - a, T], F32, tag="osb", bufs=2, name="osb")
+            nc.vector.scalar_tensor_tensor(out=osb[:], in0=o[:], scalar=OUT_SCALE,
                                            in1=b2s[:].unsqueeze(1).to_broadcast([P, b - a, T]),
                                            op0=ALU.mult, op1=ALU.add)
-            nc.sync.dma_start(out=outv[nt][:, a:b, :], in_=osb[nt][:, a:b, :])
+            nc.sync.dma_start(out=outv[nt][:, a:b, :], in_=osb[:])
+
+        def outx(nt):
+            out_from(oo[nt], nt, 0, SUB)
+
+        def out_last(h):
+            out_from(olast[h], NT - 1, 2 * h, 2 * h + 2)
 
         def w1_units(lo, hi):
             for k in range(lo, hi):
@@ -355,6 +368,8 @@ def tile_gabtemplatemlp_t_kernel(tc, seq_len, freqs, W1, b1, W2, b2, dr, dc, out
         turns(2)
 
         for per in range(1, NT + 1):
+            if per == 1:
+                w2_pe()
             mm1(per - 1, 7)
             if has(per - 2):
                 regroup(per - 2, 1)
@@ -409,9 +424,8 @@ def tile_gabtemplatemlp_t_kernel(tc, seq_len, freqs, W1, b1, W2, b2, dr, dc, out
         regroup_last(0)
         quant_part(NT - 1, 0, 0, 512)
         regroup_last(1)
-        oo[NT - 1] = ps_o.tile([P, SUB, T], F32, tag="o", name="o")
         for h in range(2):
             quant_part(NT - 1, 1, 256 * h, 256 * h + 256)
-            mm2_part(NT - 1, 2 * h, 2 * h + 2)
+            mm2_last(h)
         for h in range(2):
-            outx(NT - 1, 2 * h, 2 * h + 2)
+            out_last(h)

@@ -31,7 +31,7 @@ Z_BUFS = 7
 O_BUFS = 1
 W1_VECTOR = 6
 GP_COLS = 256
-ABS_VECTOR = 1536
+ABS_VECTOR = 1664
 PARK = PAIRS - P
 
 
@@ -355,9 +355,9 @@ def tile_gabtemplatemlp_t_kernel(tc, seq_len, freqs, W1, b1, W2, b2, dr, dc, out
         for k in range(W1_VECTOR, 16):
             w1_pe(k)
             w1_exit(k)
-        columns()
         sin_s(1)
         quant_f(0)
+        columns()
         for k in range(W1_VECTOR, 16):
             w1_quant(k)
         for j in range(4):

@@ -29,9 +29,9 @@ OUT_SCALE = 1.0 / math.sqrt(128.0)
 
 Z_BUFS = 7
 O_BUFS = 1
-W1_VECTOR = 6
-GP_COLS = 256
-ABS_VECTOR = 1664
+W1_VECTOR = 3
+GP_COLS = 320
+ABS_VECTOR = 1792
 PARK = PAIRS - P
 
 
@@ -124,7 +124,6 @@ def tile_gabtemplatemlp_t_kernel(tc, seq_len, freqs, W1, b1, W2, b2, dr, dc, out
         zz = {}
         hpl = {}
         hlast = {}
-        hgq = {}
         hgr = {}
         hq = {}
         oo = {}
@@ -132,34 +131,43 @@ def tile_gabtemplatemlp_t_kernel(tc, seq_len, freqs, W1, b1, W2, b2, dr, dc, out
         w2t = {}
         wts = {}
 
+        first = ((0, 128), (128, 256), (256, 512))
         sum0 = const.tile([P, 2, 512], F32)
-        r0 = work.tile([P, 2, 4, 256], F32, tag="r", bufs=2)
-        ab0 = work.tile([P, 2, 4, 256], F32, tag="ab", bufs=2)
+        r0 = work.tile([P, 2048], F32, tag="r", bufs=2)
+        ab0 = work.tile([P, 2048], F32, tag="ab", bufs=2)
 
-        def reduce_first(h):
-            lo, hi = 256 * h, 256 * h + 256
+        def by_type(tile, i):
+            lo, hi = first[i]
+            return tile[:, 4 * lo:4 * hi].rearrange("p (y n) -> p y n", y=4)
+
+        def reduce_first(i):
+            lo, hi = first[i]
             nc.vector.tensor_tensor(out=sum0[:, 0, lo:hi], in0=dr0[:, lo:hi], in1=dc0[:, lo:hi], op=ALU.add)
             nc.vector.tensor_tensor(out=sum0[:, 1, lo:hi], in0=dr0[:, lo:hi], in1=dc0[:, lo:hi], op=ALU.subtract)
             x = (dr0[:, lo:hi], dc0[:, lo:hi], sum0[:, 0, lo:hi], sum0[:, 1, lo:hi])
-            k0 = work.tile([P, 4, 256], I32, tag="k0", bufs=2)
+            k0 = work.tile([P, 4, hi - lo], I32, tag="k0", bufs=3)
+            r = by_type(r0, i)
             for y in range(4):
                 nc.vector.tensor_scalar(out=k0[:, y, :], in0=x[y], scalar1=fcol[:, 0:1], scalar2=None, op0=ALU.mult)
             for y in range(4):
-                nc.vector.scalar_tensor_tensor(out=r0[:, h, y, :], in0=x[y], scalar=fcol[:, 0:1], in1=k0[:, y, :],
+                nc.vector.scalar_tensor_tensor(out=r[:, y, :], in0=x[y], scalar=fcol[:, 0:1], in1=k0[:, y, :],
                                                op0=ALU.mult, op1=ALU.subtract)
 
-        def sin_first(h):
-            if h == 0:
+        def sin_first(i):
+            lo, hi = first[i]
+            if i == 0:
                 feat[0] = work.tile([P, 2, 2048], BF16, tag="f", bufs=2, align_bytes=64, name="f")
-            nc.scalar.activation(out=feat[0][:, 0, 1024 * h:1024 * h + 1024].rearrange("p (n y) -> p n y", y=4),
-                                 in_=r0[:, h, :, :].rearrange("p y n -> p n y"), func=ACT.Sin, scale=TWO_PI)
+            nc.scalar.activation(out=feat[0][:, 0, 4 * lo:4 * hi].rearrange("p (n y) -> p n y", y=4),
+                                 in_=by_type(r0, i).rearrange("p y n -> p n y"), func=ACT.Sin, scale=TWO_PI)
 
-        def fold_first(h):
-            nc.scalar.activation(out=ab0[:, h, :, :], in_=r0[:, h, :, :], func=ACT.Abs)
+        def fold_first(i):
+            lo, hi = first[i]
+            nc.scalar.activation(out=ab0[:, 4 * lo:4 * hi], in_=r0[:, 4 * lo:4 * hi], func=ACT.Abs)
 
-        def cos_first(h):
-            nc.scalar.activation(out=feat[0][:, 1, 1024 * h:1024 * h + 1024].rearrange("p (n y) -> p n y", y=4),
-                                 in_=ab0[:, h, :, :].rearrange("p y n -> p n y"), func=ACT.Sin,
+        def cos_first(i):
+            lo, hi = first[i]
+            nc.scalar.activation(out=feat[0][:, 1, 4 * lo:4 * hi].rearrange("p (n y) -> p n y", y=4),
+                                 in_=by_type(ab0, i).rearrange("p y n -> p n y"), func=ACT.Sin,
                                  scale=-TWO_PI, bias=halfpi[:])
 
         def turns(nt):
@@ -192,14 +200,13 @@ def tile_gabtemplatemlp_t_kernel(tc, seq_len, freqs, W1, b1, W2, b2, dr, dc, out
                                   in_=feat[nt][:].rearrange("p h n -> p (h n)"))
 
         def w1_pe(u):
-            j, sp = u // 2, u % 2
-            wts[u] = ps_z.tile([P, 512], BF16, tag="z", name="wt")
-            for b in range(4):
-                nc.tensor.transpose(out=wts[u][:, P * b:P * b + P],
-                                    in_=w1raw[:, 4 * j + b, P * sp:P * sp + P], identity=ident[:])
+            jj, sp = u // 2, u % 2
+            wts[u] = ps_z.tile([P, 8, P], BF16, tag="z", name="wt")
+            for b in range(8):
+                nc.tensor.transpose(out=wts[u][:, b, :], in_=w1raw[:, 8 * jj + b, P * sp:P * sp + P], identity=ident[:])
 
         def w1_exit(u):
-            wg = work.tile([P, 512], BF16, tag="wg", bufs=12, align_bytes=64)
+            wg = work.tile([P, 8, P], BF16, tag="wg", bufs=6, align_bytes=64)
             if u >= W1_VECTOR:
                 nc.scalar.copy(out=wg[:], in_=wts[u][:])
             else:
@@ -207,9 +214,10 @@ def tile_gabtemplatemlp_t_kernel(tc, seq_len, freqs, W1, b1, W2, b2, dr, dc, out
             wts[u] = wg
 
         def w1_quant(u):
-            j, sp = u // 2, u % 2
-            nc.vector.quantize_mx(out=w1c[:, sp, P * j:P * j + P].bitcast(FP8X4),
-                                  scales=w1s[:, sp, P * j:P * j + P], in_=wts[u][:])
+            jj, sp = u // 2, u % 2
+            nc.vector.quantize_mx(out=w1c[:, sp, 256 * jj:256 * jj + 256].bitcast(FP8X4),
+                                  scales=w1s[:, sp, 256 * jj:256 * jj + 256],
+                                  in_=wts[u][:].rearrange("p b q -> p (b q)"))
 
         def columns():
             bt = ps_z.tile([P, P], BF16, tag="z")
@@ -263,7 +271,7 @@ def tile_gabtemplatemlp_t_kernel(tc, seq_len, freqs, W1, b1, W2, b2, dr, dc, out
 
         def hq_tiles(nt):
             if nt not in hq:
-                hgr[nt] = work.tile([P, 2, 512, 4], BF16, tag="hg", bufs=3, align_bytes=64, name="hg")
+                hgr[nt] = work.tile([P, 2, 512, 4], BF16, tag="hg", bufs=1, align_bytes=64, name="hg")
                 hq[nt] = (work.tile([P, 2, 512], U32, tag="hc", bufs=2, align_bytes=64, name="hc"),
                           work.tile([P, 2, 512], U8, tag="hs", bufs=2, align_bytes=64, name="hs"))
 
@@ -275,19 +283,17 @@ def tile_gabtemplatemlp_t_kernel(tc, seq_len, freqs, W1, b1, W2, b2, dr, dc, out
 
         def regroup_shared(nt):
             hq_tiles(nt)
-            hgq[nt] = work.tile([P, GP_COLS, 4], BF16, tag="hgq", bufs=1, align_bytes=64, name="hgq")
-            nc.gpsimd.tensor_scalar(out=hgq[nt][:].rearrange("p (c i) t -> p c t i", i=4),
+            nc.gpsimd.tensor_scalar(out=hgr[nt][:, 0, 0:GP_COLS, :].rearrange("p (c i) t -> p c t i", i=4),
                                     in0=hpl[nt][:, 0:4, 0:GP_COLS].rearrange("p t (c i) -> p c t i", i=4),
                                     scalar1=1.0, scalar2=0.0, op0=ALU.mult, op1=ALU.add)
             nc.vector.tensor_copy(
                 out=hgr[nt][:, 0, GP_COLS:512, :].rearrange("p (c i) t -> p c t i", i=4),
                 in_=hpl[nt][:, 0:4, GP_COLS:512].rearrange("p t (c i) -> p c t i", i=4))
 
-        def quant_shared(nt):
-            quant_part(nt, 1, 0, 512)
-            quant_part(nt, 0, GP_COLS, 512)
-            nc.vector.quantize_mx(out=hq[nt][0][:, 0, 0:GP_COLS].bitcast(FP8X4), scales=hq[nt][1][:, 0, 0:GP_COLS],
-                                  in_=hgq[nt][:].rearrange("p n t -> p (n t)"))
+        def quant_h(nt):
+            nc.vector.quantize_mx(out=hq[nt][0][:].rearrange("p g n -> p (g n)").bitcast(FP8X4),
+                                  scales=hq[nt][1][:].rearrange("p g n -> p (g n)"),
+                                  in_=hgr[nt][:].rearrange("p g n t -> p (g n t)"))
 
         def quant_part(nt, g, lo, hi):
             nc.vector.quantize_mx(out=hq[nt][0][:, g, lo:hi].bitcast(FP8X4), scales=hq[nt][1][:, g, lo:hi],
@@ -339,30 +345,29 @@ def tile_gabtemplatemlp_t_kernel(tc, seq_len, freqs, W1, b1, W2, b2, dr, dc, out
         park()
         later_loads()
         nc.vector.tensor_scalar(out=fcol[:], in0=frc[:], scalar1=INV_2PI, scalar2=None, op0=ALU.mult)
-        reduce_first(0)
-        sin_first(0)
-        fold_first(0)
-        reduce_first(1)
-        cos_first(0)
-        sin_first(1)
-        fold_first(1)
+        for i in range(3):
+            reduce_first(i)
+            sin_first(i)
+            fold_first(i)
+            cos_first(i)
         w1_units(0, W1_VECTOR)
-        cos_first(1)
         turns(1)
         w1_quant(W1_VECTOR - 2)
         w1_quant(W1_VECTOR - 1)
         reduce(1)
-        for k in range(W1_VECTOR, 16):
+        for k in range(W1_VECTOR, 8):
             w1_pe(k)
             w1_exit(k)
         sin_s(1)
         quant_f(0)
         columns()
-        for k in range(W1_VECTOR, 16):
+        for k in range(W1_VECTOR, 4):
             w1_quant(k)
         for j in range(4):
             mm1(0, j)
         fold(1)
+        for k in range(4, 8):
+            w1_quant(k)
         for j in range(4, 7):
             mm1(0, j)
         turns(2)
@@ -371,49 +376,54 @@ def tile_gabtemplatemlp_t_kernel(tc, seq_len, freqs, W1, b1, W2, b2, dr, dc, out
             if per == 1:
                 w2_pe()
             mm1(per - 1, 7)
-            if has(per - 2):
-                regroup(per - 2, 1)
             if has(per + 1):
                 reduce(per + 1)
+            if has(per - 2):
+                regroup(per - 2, 1)
             if per == 1:
                 small_weights()
             if per == NT - 1:
-                quant_shared(per - 2)
+                quant_h(per - 2)
                 mm2(per - 2)
             if per == NT:
                 quant_part(per - 2, 1, 0, 512)
                 mm2(per - 2)
+            if has(per) and per > 1:
+                sin_c(per)
             silu(per - 1, 0)
             silu(per - 1, 1)
-            if has(per):
+            if per == 1:
                 sin_c(per)
             silu(per - 1, 2)
             silu(per - 1, 3)
             if has(per):
                 quant_f(per)
             if has(per - 2) and per < NT - 1:
-                quant_shared(per - 2)
+                quant_h(per - 2)
                 mm2(per - 2)
             if has(per):
                 for j in range(4):
                     mm1(per, j)
+            if per == 1:
+                silu(0, 4)
+                silu(0, 5)
             if has(per + 1):
                 sin_s(per + 1)
                 fold(per + 1)
-            if has(per - 2) and per < NT:
+            if has(per - 2) and per < NT - 1:
                 outx(per - 2)
+            if has(per + 2):
+                turns(per + 2)
             if per < NT - 1:
                 regroup_shared(per - 1)
             else:
                 regroup(per - 1, 0)
-            if per == NT:
+            if per >= NT - 1:
                 outx(per - 2)
-            if has(per + 2):
-                turns(per + 2)
             if per == NT - 1:
                 quant_part(per - 1, 0, 0, 512)
             if per < NT:
-                for j in range(4, 8):
+                for j in range(6 if per == 1 else 4, 8):
                     silu(per - 1, j)
             if has(per):
                 for j in range(4, 7):

from contextlib import ExitStack
import math

import concourse.mybir as mybir
from concourse.masks import make_identity

F32 = mybir.dt.float32
BF16 = mybir.dt.bfloat16
I32 = mybir.dt.int32
U32 = mybir.dt.uint32
U8 = mybir.dt.uint8
FP8X4 = mybir.dt.float8_e4m3fn_x4
ALU = mybir.AluOpType
ACT = mybir.ActivationFunctionType

P = 128
PAIRS = 4096
NT = 8
SUB = 4
NCH = NT * SUB
HID = 1024
MT = 8
T = 128
FLOPS = 2 * PAIRS * 1024 * HID + 2 * PAIRS * HID * T

INV_2PI = 1.0 / (2.0 * math.pi)
TWO_PI = 2.0 * math.pi
OUT_SCALE = 1.0 / math.sqrt(128.0)

Z_BUFS = 7
O_BUFS = 1
W1_VECTOR = 3
GP_COLS = 320
ABS_VECTOR = 1792
PARK = PAIRS - P


def tile_gabtemplatemlp_t_kernel(tc, seq_len, freqs, W1, b1, W2, b2, dr, dc, out):
    nc = tc.nc
    with ExitStack() as ctx:
        ctx.enter_context(tc.manual_schedule())
        const = ctx.enter_context(tc.tile_pool(name="const", bufs=1))
        work = ctx.enter_context(tc.tile_pool(name="work", bufs=2))
        ps_z = ctx.enter_context(tc.psum_pool(name="ps_z", bufs=Z_BUFS))
        ps_o = ctx.enter_context(tc.psum_pool(name="ps_o", bufs=O_BUFS))

        drf = dr.rearrange("i j -> (i j)")
        dcf = dc.rearrange("i j -> (i j)")
        drc = const.tile([P, 32], BF16)
        nc.sync.dma_start(out=drc[:], in_=drf.rearrange("(q n) -> q n", n=32))
        dcc = const.tile([P, 32], BF16)
        nc.sync.dma_start(out=dcc[:], in_=dcf.rearrange("(q n) -> q n", n=32))
        frc = const.tile([P, 1], BF16)
        nc.sync.dma_start(out=frc[:], in_=freqs.rearrange("(p o) -> p o", o=1))
        dr0 = const.tile([P, 512], BF16)
        nc.sync.dma_start(out=dr0[:], in_=drf[0:512].partition_broadcast(P))
        dc0 = const.tile([P, 512], BF16)
        nc.sync.dma_start(out=dc0[:], in_=dcf[0:512].partition_broadcast(P))
        w1raw = const.tile([P, 32, 256], BF16)
        w1v = W1.rearrange("h f -> (h f)").rearrange("(b q x) -> q b x", q=P, x=256)
        brow = const.tile([P, P], BF16)
        nc.gpsimd.memset(brow[:], 0.0)

        def load_w1(part):
            nc.sync.dma_start(out=w1raw[:, 8 * part:8 * part + 8, :], in_=w1v[:, 8 * part:8 * part + 8, :])

        load_w1(0)
        warm = const.tile([P, 1], F32)
        nc.vector.memset(warm[:], 0.0)
        nc.scalar.activation(out=warm[:], in_=warm[:], func=ACT.Silu)

        x4 = const.tile([P, 32, 4], F32)
        rows = out.rearrange("i j t -> (i j) t")
        parked = rows[PARK:PAIRS, :].rearrange("q x -> (q x)")
        xs = {}

        def park():
            nc.vector.tensor_copy(out=x4[:, :, 0], in_=drc[:])
            nc.vector.tensor_copy(out=x4[:, :, 1], in_=dcc[:])
            nc.vector.tensor_tensor(out=x4[:, :, 2], in0=drc[:], in1=dcc[:], op=ALU.add)
            nc.vector.tensor_tensor(out=x4[:, :, 3], in0=drc[:], in1=dcc[:], op=ALU.subtract)
            nc.sync.dma_start(out=rows[PARK:PAIRS, :], in_=x4[:].rearrange("q n t -> q (n t)"))

        def load_x(a):
            xs[a] = work.tile([P, 2048], F32, tag="x", bufs=4, name="x")
            nc.sync.dma_start(out=xs[a][:], in_=parked[2048 * a:2048 * a + 2048].partition_broadcast(P))

        w2raw = const.tile([P, HID], BF16)
        b2b = const.tile([P, T], BF16)

        def later_loads():
            load_w1(1)
            load_w1(2)
            load_x(1)
            load_w1(3)
            nc.sync.dma_start(out=brow[0:8, :], in_=b1.rearrange("(j p) -> j p", p=P))
            nc.sync.dma_start(out=w2raw[:], in_=W2)
            load_x(2)
            nc.sync.dma_start(out=b2b[:], in_=b2.partition_broadcast(P))
            for a in range(3, NT):
                load_x(a)

        ident = const.tile([P, P], BF16)
        make_identity(nc, ident[:])
        one = const.tile([P, 1], F32)
        nc.vector.memset(one[:], 1.0)
        halfpi = const.tile([P, 1], F32)
        nc.vector.tensor_scalar(out=halfpi[:], in0=one[:], scalar1=math.pi / 2.0, scalar2=None, op0=ALU.mult)

        w1c = const.tile([P, 2, HID], U32, align_bytes=64)
        w1s = const.tile([P, 2, HID], U8, align_bytes=64)
        w2c = const.tile([P, 2, T], U32, align_bytes=64)
        w2s = const.tile([P, 2, T], U8, align_bytes=64)
        b1c = const.tile([P, MT], F32)
        fcol = const.tile([P, 1], F32)
        b2s = const.tile([P, T], F32)
        outv = rows.rearrange("(a s n) t -> a n s t", n=P, s=SUB)

        kk = {}
        rr = {}
        fq = {}
        ab = {}
        feat = {}
        zz = {}
        hpl = {}
        hlast = {}
        hgr = {}
        hq = {}
        oo = {}
        olast = {}
        w2t = {}
        wts = {}

        first = ((0, 128), (128, 256), (256, 512))
        sum0 = const.tile([P, 2, 512], F32)
        r0 = work.tile([P, 2048], F32, tag="r", bufs=2)
        ab0 = work.tile([P, 2048], F32, tag="ab", bufs=2)

        def by_type(tile, i):
            lo, hi = first[i]
            return tile[:, 4 * lo:4 * hi].rearrange("p (y n) -> p y n", y=4)

        def reduce_first(i):
            lo, hi = first[i]
            nc.vector.tensor_tensor(out=sum0[:, 0, lo:hi], in0=dr0[:, lo:hi], in1=dc0[:, lo:hi], op=ALU.add)
            nc.vector.tensor_tensor(out=sum0[:, 1, lo:hi], in0=dr0[:, lo:hi], in1=dc0[:, lo:hi], op=ALU.subtract)
            x = (dr0[:, lo:hi], dc0[:, lo:hi], sum0[:, 0, lo:hi], sum0[:, 1, lo:hi])
            k0 = work.tile([P, 4, hi - lo], I32, tag="k0", bufs=3)
            r = by_type(r0, i)
            for y in range(4):
                nc.vector.tensor_scalar(out=k0[:, y, :], in0=x[y], scalar1=fcol[:, 0:1], scalar2=None, op0=ALU.mult)
            for y in range(4):
                nc.vector.scalar_tensor_tensor(out=r[:, y, :], in0=x[y], scalar=fcol[:, 0:1], in1=k0[:, y, :],
                                               op0=ALU.mult, op1=ALU.subtract)

        def sin_first(i):
            lo, hi = first[i]
            if i == 0:
                feat[0] = work.tile([P, 2, 2048], BF16, tag="f", bufs=2, align_bytes=64, name="f")
            nc.scalar.activation(out=feat[0][:, 0, 4 * lo:4 * hi].rearrange("p (n y) -> p n y", y=4),
                                 in_=by_type(r0, i).rearrange("p y n -> p n y"), func=ACT.Sin, scale=TWO_PI)

        def fold_first(i):
            lo, hi = first[i]
            nc.scalar.activation(out=ab0[:, 4 * lo:4 * hi], in_=r0[:, 4 * lo:4 * hi], func=ACT.Abs)

        def cos_first(i):
            lo, hi = first[i]
            nc.scalar.activation(out=feat[0][:, 1, 4 * lo:4 * hi].rearrange("p (n y) -> p n y", y=4),
                                 in_=by_type(ab0, i).rearrange("p y n -> p n y"), func=ACT.Sin,
                                 scale=-TWO_PI, bias=halfpi[:])

        def turns(nt):
            kk[nt] = work.tile([P, 2048], I32, tag="kk", bufs=2, name="kk")
            nc.vector.tensor_scalar(out=kk[nt][:], in0=xs[nt][:], scalar1=fcol[:, 0:1], scalar2=None, op0=ALU.mult)

        def reduce(nt):
            rr[nt] = work.tile([P, 2048], F32, tag="r", bufs=2, name="r")
            nc.vector.scalar_tensor_tensor(out=rr[nt][:], in0=xs[nt][:], scalar=fcol[:, 0:1], in1=kk[nt][:],
                                           op0=ALU.mult, op1=ALU.subtract)

        def sin_s(nt):
            feat[nt] = work.tile([P, 2, 2048], BF16, tag="f", bufs=2, align_bytes=64, name="f")
            nc.scalar.activation(out=feat[nt][:, 0, :], in_=rr[nt][:], func=ACT.Sin, scale=TWO_PI)

        def fold(nt):
            ab[nt] = work.tile([P, 2048], F32, tag="ab", bufs=2, name="ab")
            nc.vector.tensor_reduce(out=ab[nt][:, 0:ABS_VECTOR], in_=rr[nt][:, 0:ABS_VECTOR].unsqueeze(2),
                                    axis=mybir.AxisListType.X, op=ALU.max, apply_absolute_value=True)
            nc.scalar.activation(out=ab[nt][:, ABS_VECTOR:2048], in_=rr[nt][:, ABS_VECTOR:2048], func=ACT.Abs)

        def sin_c(nt):
            nc.scalar.activation(out=feat[nt][:, 1, :], in_=ab[nt][:], func=ACT.Sin, scale=-TWO_PI, bias=halfpi[:])

        def quant_f(nt):
            fq[nt] = (work.tile([P, 2, 512], U32, tag="fqc", bufs=2, align_bytes=64, name="fqc"),
                      work.tile([P, 2, 512], U8, tag="fqs", bufs=2, align_bytes=64, name="fqs"))
            nc.vector.quantize_mx(out=fq[nt][0][:].rearrange("p h n -> p (h n)").bitcast(FP8X4),
                                  scales=fq[nt][1][:].rearrange("p h n -> p (h n)"),
                                  in_=feat[nt][:].rearrange("p h n -> p (h n)"))

        def w1_pe(u):
            jj, sp = u // 2, u % 2
            wts[u] = ps_z.tile([P, 8, P], BF16, tag="z", name="wt")
            for b in range(8):
                nc.tensor.transpose(out=wts[u][:, b, :], in_=w1raw[:, 8 * jj + b, P * sp:P * sp + P], identity=ident[:])

        def w1_exit(u):
            wg = work.tile([P, 8, P], BF16, tag="wg", bufs=6, align_bytes=64)
            if u >= W1_VECTOR:
                nc.scalar.copy(out=wg[:], in_=wts[u][:])
            else:
                nc.vector.tensor_copy(out=wg[:], in_=wts[u][:])
            wts[u] = wg

        def w1_quant(u):
            jj, sp = u // 2, u % 2
            nc.vector.quantize_mx(out=w1c[:, sp, 256 * jj:256 * jj + 256].bitcast(FP8X4),
                                  scales=w1s[:, sp, 256 * jj:256 * jj + 256],
                                  in_=wts[u][:].rearrange("p b q -> p (b q)"))

        def columns():
            bt = ps_z.tile([P, P], BF16, tag="z")
            nc.tensor.transpose(out=bt[:], in_=brow[:], identity=ident[:])
            nc.vector.tensor_copy(out=b1c[:], in_=bt[:, 0:MT])

        def w2_pe():
            for g in range(2):
                w2t[g] = ps_z.tile([P, 4, P], BF16, tag="z", name="w2t")
                for t in range(4):
                    nc.tensor.transpose(out=w2t[g][:, t, :], in_=w2raw[:, P * (4 * g + t):P * (4 * g + t) + P],
                                        identity=ident[:])

        def small_weights():
            nc.vector.tensor_scalar(out=b2s[:], in0=b2b[:], scalar1=OUT_SCALE, scalar2=None, op0=ALU.mult)
            w2g = {}
            for g in range(2):
                w2g[g] = work.tile([P, P, 4], BF16, tag="w2g", bufs=2, align_bytes=64, name="w2g")
                nc.vector.tensor_copy(out=w2g[g][:], in_=w2t[g][:].rearrange("p t c -> p c t"))
            for g in range(2):
                nc.vector.quantize_mx(out=w2c[:, g, :].bitcast(FP8X4), scales=w2s[:, g, :],
                                      in_=w2g[g][:].rearrange("p c t -> p (c t)"))

        def mm1(nt, j):
            zz[(nt, j)] = ps_z.tile([P, 512], F32, tag="z", name="z")
            for sp in range(2):
                nc.tensor.matmul_mx(
                    out=zz[(nt, j)][:],
                    lhsT=w1c[:, sp, P * j:P * j + P].bitcast(FP8X4),
                    lhsT_scale=w1s[:, sp, P * j:P * j + P],
                    rhs=fq[nt][0][:, sp, :].bitcast(FP8X4),
                    rhs_scale=fq[nt][1][:, sp, :],
                    start=(sp == 0), stop=(sp == 1),
                )

        def silu(nt, j):
            if nt not in hpl:
                hpl[nt] = work.tile([P, MT, 512], BF16, tag="hpl", bufs=2, name="hpl")
            nc.scalar.activation(out=hpl[nt][:, j, :], in_=zz[(nt, j)][:], func=ACT.Silu, bias=b1c[:, j:j + 1])

        def silu_last(h, j):
            if h not in hlast:
                hlast[h] = work.tile([P, 4, 256], BF16, tag="hlast", bufs=2, name="hlast")
            nc.scalar.activation(out=hlast[h][:, j - 4, :], in_=zz[(NT - 1, j)][:, 256 * h:256 * h + 256], func=ACT.Silu,
                                 bias=b1c[:, j:j + 1])

        def regroup_last(h):
            nc.vector.tensor_copy(
                out=hgr[NT - 1][:, 1, 256 * h:256 * h + 256, :].rearrange("p (c i) t -> p c t i", i=4),
                in_=hlast[h][:].rearrange("p t (c i) -> p c t i", i=4))

        def hq_tiles(nt):
            if nt not in hq:
                hgr[nt] = work.tile([P, 2, 512, 4], BF16, tag="hg", bufs=1, align_bytes=64, name="hg")
                hq[nt] = (work.tile([P, 2, 512], U32, tag="hc", bufs=2, align_bytes=64, name="hc"),
                          work.tile([P, 2, 512], U8, tag="hs", bufs=2, align_bytes=64, name="hs"))

        def regroup(nt, g):
            hq_tiles(nt)
            nc.vector.tensor_copy(
                out=hgr[nt][:, g, :, :].rearrange("p (c i) t -> p c t i", i=4),
                in_=hpl[nt][:, 4 * g:4 * g + 4, :].rearrange("p t (c i) -> p c t i", i=4))

        def regroup_shared(nt):
            hq_tiles(nt)
            nc.gpsimd.tensor_scalar(out=hgr[nt][:, 0, 0:GP_COLS, :].rearrange("p (c i) t -> p c t i", i=4),
                                    in0=hpl[nt][:, 0:4, 0:GP_COLS].rearrange("p t (c i) -> p c t i", i=4),
                                    scalar1=1.0, scalar2=0.0, op0=ALU.mult, op1=ALU.add)
            nc.vector.tensor_copy(
                out=hgr[nt][:, 0, GP_COLS:512, :].rearrange("p (c i) t -> p c t i", i=4),
                in_=hpl[nt][:, 0:4, GP_COLS:512].rearrange("p t (c i) -> p c t i", i=4))

        def quant_h(nt):
            nc.vector.quantize_mx(out=hq[nt][0][:].rearrange("p g n -> p (g n)").bitcast(FP8X4),
                                  scales=hq[nt][1][:].rearrange("p g n -> p (g n)"),
                                  in_=hgr[nt][:].rearrange("p g n t -> p (g n t)"))

        def quant_part(nt, g, lo, hi):
            nc.vector.quantize_mx(out=hq[nt][0][:, g, lo:hi].bitcast(FP8X4), scales=hq[nt][1][:, g, lo:hi],
                                  in_=hgr[nt][:, g, lo:hi, :].rearrange("p n t -> p (n t)"))

        def mm2(nt):
            oo[nt] = ps_o.tile([P, SUB, T], F32, tag="o", name="o")
            mm2_into(oo[nt], nt, 0, SUB)

        def mm2_last(h):
            olast[h] = ps_z.tile([P, 2, T], F32, tag="z", name="olast")
            mm2_into(olast[h], NT - 1, 2 * h, 2 * h + 2)

        def mm2_into(o, nt, a, b):
            for s in range(a, b):
                for g in range(2):
                    nc.tensor.matmul_mx(
                        out=o[:, s - a, :],
                        lhsT=hq[nt][0][:, g, P * s:P * s + P].bitcast(FP8X4),
                        lhsT_scale=hq[nt][1][:, g, P * s:P * s + P],
                        rhs=w2c[:, g, :].bitcast(FP8X4),
                        rhs_scale=w2s[:, g, :],
                        start=(g == 0), stop=(g == 1),
                    )

        def out_from(o, nt, a, b):
            osb = work.tile([P, b - a, T], F32, tag="osb", bufs=2, name="osb")
            nc.vector.scalar_tensor_tensor(out=osb[:], in0=o[:], scalar=OUT_SCALE,
                                           in1=b2s[:].unsqueeze(1).to_broadcast([P, b - a, T]),
                                           op0=ALU.mult, op1=ALU.add)
            nc.sync.dma_start(out=outv[nt][:, a:b, :], in_=osb[:])

        def outx(nt):
            out_from(oo[nt], nt, 0, SUB)

        def out_last(h):
            out_from(olast[h], NT - 1, 2 * h, 2 * h + 2)

        def w1_units(lo, hi):
            for k in range(lo, hi):
                w1_pe(k)
                w1_exit(k)
                if k >= 2:
                    w1_quant(k - 2)

        def has(nt):
            return 0 <= nt < NT

        park()
        later_loads()
        nc.vector.tensor_scalar(out=fcol[:], in0=frc[:], scalar1=INV_2PI, scalar2=None, op0=ALU.mult)
        for i in range(3):
            reduce_first(i)
            sin_first(i)
            fold_first(i)
            cos_first(i)
        w1_units(0, W1_VECTOR)
        turns(1)
        w1_quant(W1_VECTOR - 2)
        w1_quant(W1_VECTOR - 1)
        reduce(1)
        for k in range(W1_VECTOR, 8):
            w1_pe(k)
            w1_exit(k)
        sin_s(1)
        quant_f(0)
        columns()
        for k in range(W1_VECTOR, 4):
            w1_quant(k)
        for j in range(4):
            mm1(0, j)
        fold(1)
        for k in range(4, 8):
            w1_quant(k)
        for j in range(4, 7):
            mm1(0, j)
        turns(2)

        for per in range(1, NT + 1):
            if per == 1:
                w2_pe()
            mm1(per - 1, 7)
            if has(per + 1):
                reduce(per + 1)
            if has(per - 2):
                regroup(per - 2, 1)
            if per == 1:
                small_weights()
            if per == NT - 1:
                quant_h(per - 2)
                mm2(per - 2)
            if per == NT:
                quant_part(per - 2, 1, 0, 512)
                mm2(per - 2)
            if has(per) and per > 1:
                sin_c(per)
            silu(per - 1, 0)
            silu(per - 1, 1)
            if per == 1:
                sin_c(per)
            silu(per - 1, 2)
            silu(per - 1, 3)
            if has(per):
                quant_f(per)
            if has(per - 2) and per < NT - 1:
                quant_h(per - 2)
                mm2(per - 2)
            if has(per):
                for j in range(4):
                    mm1(per, j)
            if per == 1:
                silu(0, 4)
                silu(0, 5)
            if has(per + 1):
                sin_s(per + 1)
                fold(per + 1)
            if has(per - 2) and per < NT - 1:
                outx(per - 2)
            if has(per + 2):
                turns(per + 2)
            if per < NT - 1:
                regroup_shared(per - 1)
            else:
                regroup(per - 1, 0)
            if per >= NT - 1:
                outx(per - 2)
            if per == NT - 1:
                quant_part(per - 1, 0, 0, 512)
            if per < NT:
                for j in range(6 if per == 1 else 4, 8):
                    silu(per - 1, j)
            if has(per):
                for j in range(4, 7):
                    mm1(per, j)
        for h in range(2):
            for j in range(4, 8):
                silu_last(h, j)
        regroup_last(0)
        quant_part(NT - 1, 0, 0, 512)
        regroup_last(1)
        for h in range(2):
            quant_part(NT - 1, 1, 256 * h, 256 * h + 256)
            mm2_last(h)
        for h in range(2):
            out_last(h)
